import numpy as np
import ml_dtypes


def mxq(x, axis, fmt="e4m3"):
    dtype, down = {"e4m3": (ml_dtypes.float8_e4m3fn, 7), "e5m2": (ml_dtypes.float8_e5m2, 14)}[fmt]
    v = np.moveaxis(np.asarray(x, np.float32).astype(ml_dtypes.bfloat16).astype(np.float64), axis, -1)
    blocks = v.reshape(v.shape[:-1] + (-1, 32))
    amax = np.abs(blocks).max(-1, keepdims=True)
    byte = np.maximum(np.where(amax > 0, np.frexp(amax)[1] - 1 + 127, 0) - down, 1)
    scale = np.exp2(byte - 127.0)
    codes = (blocks / scale).astype(np.float32).astype(dtype).astype(np.float64)
    return np.moveaxis((codes * scale).reshape(v.shape), -1, axis)


WIDE = False


def mx_kscale(k):
    if not WIDE:
        return np.ones(k)
    levels = np.array([10, -10, 5, -5, 0])
    a = np.random.permutation(np.resize(levels, k // 512 * 4)).reshape(k // 512, 4)
    idx = np.arange(k)
    return np.exp2(a[idx // 512, idx % 128 // 32])


BF16 = ml_dtypes.bfloat16


def bf(x):
    return np.asarray(x, np.float32).astype(BF16)


def f64(x):
    return np.asarray(x).astype(np.float64)


B, I, J, P = 256, 8192, 128, 8
TEMP = 1.0


def primitives(x):
    return np.stack([np.zeros_like(x), x, x * x, x * x * x, np.exp(x), np.log(x), 1.0 / x, np.sin(x)], axis=-1)


def setup_inputs():
    r = np.exp2(np.round(np.log2(mx_kscale(I)) / 3))
    g = np.exp2(np.round(1.5 * (r - 1.0) / np.log(2.0)))
    one = np.ones(I)
    undo = np.stack([one, 1.0 / r, 1.0 / r**2, 1.0 / r**3, 1.0 / g, one, r, one], axis=-1)
    return {"x": bf((np.random.random_sample((B, I)) + 0.5) * r),
            "alphas": bf(np.random.standard_normal((I, J, P))),
            "coeffs": bf(np.random.standard_normal((I, J, P)) * 3.0 / np.sqrt(I) * undo[:, None, :])}


def reference(x, alphas, coeffs):
    a = f64(alphas) / TEMP
    e = np.exp(a - a.max(-1, keepdims=True))
    gates = e / e.sum(-1, keepdims=True)
    prims = primitives(f64(x))
    w = gates * f64(coeffs)
    p = prims[:, :, 1:].transpose(2, 0, 1)
    v = w[:, :, 1:].transpose(2, 0, 1)
    return (mxq(p, 2, "e4m3") @ mxq(v, 1, "e4m3")).sum(0)

@@ -1,0 +1,271 @@
+import math
+from contextlib import ExitStack
+
+import concourse.mybir as mybir
+from concourse.masks import make_identity
+
+BF16 = mybir.dt.bfloat16
+F32 = mybir.dt.float32
+U32 = mybir.dt.uint32
+U8 = mybir.dt.uint8
+FP8X4 = mybir.dt.float8_e4m3fn_x4
+ACT = mybir.ActivationFunctionType
+ALU = mybir.AluOpType
+
+B, I, J, PRIMS = 256, 8192, 128, 8
+CHANNELS = PRIMS - 1
+P = 128
+PACK = 4
+K_PASS = P * PACK
+PASSES = 2
+I_BATCH = PASSES * K_PASS
+BATCHES = I // I_BATCH
+HALVES = B // P
+GROUPS = PASSES * J * PACK
+X_COLS = PASSES * B * PACK
+
+FLOPS = 2 * B * J * I * CHANNELS
+
+
+def tile_dartslayer_k_kernel(tc, x, alphas, coeffs, out):
+    nc = tc.nc
+    with ExitStack() as ctx:
+        sbuf = ctx.enter_context(tc.tile_pool(name="sbuf", bufs=1))
+        psum = ctx.enter_context(tc.psum_pool(name="psum", bufs=1))
+
+        identity = sbuf.tile([P, P], F32)
+        make_identity(nc, identity[:])
+        zero = sbuf.tile([P, 1], F32)
+        nc.vector.memset(zero[:], 0.0)
+        fold_shift = sbuf.tile([P, 3], F32)
+        for place, turns in enumerate((2.5, 1.0, 0.5)):
+            nc.vector.tensor_scalar_add(
+                out=fold_shift[:, place : place + 1], in0=zero[:], scalar1=-turns * math.pi
+            )
+
+        acc = []
+        for h in range(HALVES):
+            acc_h = psum.tile([P, J], F32, name="acc%d" % h)
+            acc.append(acc_h)
+
+        x_rows_of, x_t_of, ln_x_of, alpha_of, coeff_of = {}, {}, {}, {}, {}
+        gate_of, total_of, prim_of, folded_of, p_mx_of, w_mx_of = {}, {}, {}, {}, {}, {}
+
+        def load_x(n):
+            x_rows = sbuf.tile([P, HALVES, I_BATCH], BF16, bufs=2)
+            nc.sync.dma_start(
+                out=x_rows[:],
+                in_=x[:, n * I_BATCH : (n + 1) * I_BATCH].rearrange("(h b) i -> b h i", h=HALVES),
+            )
+            x_rows_of[n] = x_rows
+
+        def load_weights(n, source, tiles, label):
+            rows = sbuf.tile([P, PASSES, PACK, J, PRIMS], BF16, name=label)
+            nc.sync.dma_start(
+                out=rows[:].rearrange("p c t j k -> p c (t j k)"),
+                in_=source[n * I_BATCH : (n + 1) * I_BATCH].rearrange(
+                    "(c p t) j k -> p c (t j k)", c=PASSES, p=P, t=PACK
+                ),
+            )
+            tiles[n] = rows
+
+        def transpose_x(n):
+            words = x_rows_of[n][:].bitcast(F32)
+            x_t = sbuf.tile([P, PASSES, B, PACK], BF16, bufs=2, align_bytes=64)
+            x_t_words = x_t[:].bitcast(F32)
+            pass_words = K_PASS // 2
+            for c in range(PASSES):
+                turned = psum.tile([P, HALVES, 2, P], F32, bufs=2)
+                for h in range(HALVES):
+                    for u in range(2):
+                        nc.tensor.transpose(
+                            turned[:, h, u, :],
+                            words[:, h, c * pass_words + u : (c + 1) * pass_words : 2],
+                            identity[:],
+                        )
+                nc.scalar.copy(
+                    out=x_t_words[:, c].rearrange("p (h b) u -> p h b u", h=HALVES),
+                    in_=turned[:].rearrange("p h u b -> p h b u"),
+                )
+            x_t_of[n] = x_t
+
+        def log_x(n):
+            ln_x = sbuf.tile([P, X_COLS], F32)
+            nc.scalar.activation(
+                out=ln_x[:], in_=x_t_of[n][:].rearrange("p c b t -> p (c b t)"), func=ACT.Ln
+            )
+            ln_x_of[n] = ln_x
+
+        def shift(n):
+            rows = alpha_of[n]
+            by_group = rows[:].rearrange("p c t j k -> p (c t j) k")
+            max4 = sbuf.tile([P, GROUPS, 4], BF16)
+            max2 = sbuf.tile([P, GROUPS, 2], BF16)
+            max1 = sbuf.tile([P, PASSES, PACK, J, 1], BF16)
+            nc.vector.tensor_tensor(
+                out=max4[:], in0=by_group[:, :, 0:4], in1=by_group[:, :, 4:8], op=ALU.max
+            )
+            nc.vector.tensor_tensor(
+                out=max2[:], in0=max4[:, :, 0:2], in1=max4[:, :, 2:4], op=ALU.max
+            )
+            nc.vector.tensor_tensor(
+                out=max1[:].rearrange("p c t j o -> p (c t j) o"),
+                in0=max2[:, :, 0:1],
+                in1=max2[:, :, 1:2],
+                op=ALU.max,
+            )
+            gate = sbuf.tile([P, PASSES, J, PACK, PRIMS], F32, bufs=2)
+            for c in range(PASSES):
+                nc.vector.tensor_tensor(
+                    out=gate[:, c],
+                    in0=rows[:, c].rearrange("p t j k -> p j t k"),
+                    in1=max1[:, c].rearrange("p t j o -> p j t o").to_broadcast([P, J, PACK, PRIMS]),
+                    op=ALU.subtract,
+                )
+            gate_of[n] = gate
+
+        def exponential(n):
+            flat = gate_of[n][:].rearrange("p c j t k -> p (c j t k)")
+            nc.scalar.activation(out=flat, in_=flat, func=ACT.Exp)
+
+        def total(n):
+            sums = sbuf.tile([P, GROUPS], F32)
+            nc.vector.tensor_reduce(
+                out=sums[:],
+                in_=gate_of[n][:].rearrange("p c j t k -> p (c j t) k"),
+                axis=mybir.AxisListType.X,
+                op=ALU.add,
+            )
+            total_of[n] = sums
+
+        def times_coeffs(n):
+            gate = gate_of[n]
+            for c in range(PASSES):
+                nc.vector.tensor_tensor(
+                    out=gate[:, c, :, :, 1:PRIMS],
+                    in0=gate[:, c, :, :, 1:PRIMS],
+                    in1=coeff_of[n][:, c].rearrange("p t j k -> p j t k")[:, :, :, 1:PRIMS],
+                    op=ALU.mult,
+                )
+
+        def primitives_exp_set(n):
+            x_t = x_t_of[n][:].rearrange("p c b t -> p (c b t)")
+            ln_x = ln_x_of[n]
+            square = sbuf.tile([P, X_COLS], BF16, align_bytes=64)
+            cube = sbuf.tile([P, X_COLS], BF16, align_bytes=64)
+            exp_x = sbuf.tile([P, X_COLS], BF16, align_bytes=64)
+            log_bf = sbuf.tile([P, X_COLS], BF16, align_bytes=64)
+            inverse = sbuf.tile([P, X_COLS], BF16, align_bytes=64)
+            folded = sbuf.tile([P, X_COLS], F32)
+            nc.scalar.copy(out=log_bf[:], in_=ln_x[:])
+            nc.scalar.activation(out=inverse[:], in_=ln_x[:], func=ACT.Exp, scale=-1.0)
+            nc.scalar.activation(out=cube[:], in_=ln_x[:], func=ACT.Exp, scale=3.0)
+            nc.scalar.activation(out=exp_x[:], in_=x_t, func=ACT.Exp)
+            nc.scalar.activation(out=square[:], in_=x_t, func=ACT.Square)
+            nc.scalar.activation(out=folded[:], in_=x_t, func=ACT.Abs, bias=fold_shift[:, 0:1])
+            nc.scalar.activation(out=folded[:], in_=folded[:], func=ACT.Abs, bias=fold_shift[:, 1:2])
+            prim_of[n] = [x_t, square[:], cube[:], exp_x[:], log_bf[:], inverse[:]]
+            folded_of[n] = folded
+
+        def primitive_sin(n):
+            sine = sbuf.tile([P, X_COLS], BF16, align_bytes=64)
+            nc.scalar.activation(
+                out=sine[:], in_=folded_of[n][:], func=ACT.Sin, bias=fold_shift[:, 2:3]
+            )
+            prim_of[n].append(sine[:])
+
+        def log_total(n):
+            nc.scalar.activation(out=total_of[n][:], in_=total_of[n][:], func=ACT.Ln)
+
+        def reciprocal_total(n):
+            nc.scalar.activation(out=total_of[n][:], in_=total_of[n][:], func=ACT.Exp, scale=-1.0)
+
+        def quantise_x(n):
+            p_codes = sbuf.tile([P, CHANNELS, PASSES, B], U32, align_bytes=64)
+            p_scales = sbuf.tile([P, CHANNELS, PASSES, B], U8, align_bytes=64)
+            for ch in range(CHANNELS):
+                nc.vector.quantize_mx(
+                    out=p_codes[:, ch].rearrange("p c b -> p (c b)").bitcast(FP8X4),
+                    scales=p_scales[:, ch].rearrange("p c b -> p (c b)"),
+                    in_=prim_of[n][ch],
+                )
+            p_mx_of[n] = (p_codes, p_scales)
+
+        def normalise(n):
+            by_group = gate_of[n][:].rearrange("p c j t k -> p (c j t) k")
+            w = sbuf.tile([P, CHANNELS, GROUPS], BF16, align_bytes=64)
+            for k_lo, k_hi in ((1, 4), (4, 8)):
+                nc.vector.tensor_tensor(
+                    out=w[:, k_lo - 1 : k_hi - 1, :].rearrange("p k g -> p g k"),
+                    in0=by_group[:, :, k_lo:k_hi],
+                    in1=total_of[n][:].unsqueeze(2).to_broadcast([P, GROUPS, k_hi - k_lo]),
+                    op=ALU.mult,
+                )
+            w_codes = sbuf.tile([P, CHANNELS, PASSES, J], U32, align_bytes=64)
+            w_scales = sbuf.tile([P, CHANNELS, PASSES, J], U8, align_bytes=64)
+            for ch in range(CHANNELS):
+                nc.vector.quantize_mx(
+                    out=w_codes[:, ch].rearrange("p c j -> p (c j)").bitcast(FP8X4),
+                    scales=w_scales[:, ch].rearrange("p c j -> p (c j)"),
+                    in_=w[:, ch, :],
+                )
+            w_mx_of[n] = (w_codes, w_scales)
+
+        def multiply(n):
+            p_codes, p_scales = p_mx_of[n]
+            w_codes, w_scales = w_mx_of[n]
+            for c in range(PASSES):
+                for ch in range(CHANNELS):
+                    first = n == 0 and c == 0 and ch == 0
+                    last = n == BATCHES - 1 and c == PASSES - 1 and ch == CHANNELS - 1
+                    for h in range(HALVES):
+                        rows = slice(h * P, (h + 1) * P)
+                        nc.tensor.matmul_mx(
+                            out=acc[h][:],
+                            lhsT=p_codes[:, ch, c, rows].bitcast(FP8X4),
+                            lhsT_scale=p_scales[:, ch, c, rows],
+                            rhs=w_codes[:, ch, c, :].bitcast(FP8X4),
+                            rhs_scale=w_scales[:, ch, c, :],
+                            start=first,
+                            stop=last,
+                        )
+
+        with tc.manual_schedule():
+            load_x(0)
+            load_weights(0, alphas, alpha_of, "alpha_rows")
+            load_weights(0, coeffs, coeff_of, "coeff_rows")
+            load_x(1)
+            transpose_x(0)
+            log_x(0)
+            shift(0)
+            load_weights(1, alphas, alpha_of, "alpha_rows")
+            for n in range(BATCHES):
+                if n > 0:
+                    reciprocal_total(n - 1)
+                    normalise(n - 1)
+                    multiply(n - 1)
+                exponential(n)
+                total(n)
+                times_coeffs(n)
+                if n + 1 < BATCHES:
+                    load_weights(n + 1, coeffs, coeff_of, "coeff_rows")
+                primitives_exp_set(n)
+                primitive_sin(n)
+                if n + 1 < BATCHES:
+                    shift(n + 1)
+                if n + 2 < BATCHES:
+                    load_weights(n + 2, alphas, alpha_of, "alpha_rows")
+                log_total(n)
+                if n + 1 < BATCHES:
+                    transpose_x(n + 1)
+                    log_x(n + 1)
+                if n + 2 < BATCHES:
+                    load_x(n + 2)
+                quantise_x(n)
+            reciprocal_total(BATCHES - 1)
+            normalise(BATCHES - 1)
+            multiply(BATCHES - 1)
+            for h in range(HALVES):
+                result = sbuf.tile([P, J], F32, bufs=2)
+                nc.vector.tensor_copy(out=result[:], in_=acc[h][:])
+                nc.sync.dma_start(out=out[h * P : (h + 1) * P, :], in_=result[:])

@@ -23,6 +23,8 @@ BATCHES = I // I_BATCH
 HALVES = B // P
 GROUPS = PASSES * J * PACK
 X_COLS = PASSES * B * PACK
+PASS_GROUPS = J * PACK
+BLOCKS = PASS_GROUPS // P
 
 FLOPS = 2 * B * J * I * CHANNELS
 
@@ -50,6 +52,7 @@ def tile_dartslayer_k_kernel(tc, x, alphas, coeffs, out):
 
         x_rows_of, x_t_of, ln_x_of, alpha_of, coeff_of = {}, {}, {}, {}, {}
         gate_of, total_of, prim_of, folded_of, p_mx_of, w_mx_of = {}, {}, {}, {}, {}, {}
+        recip_t_of, recip_of = {}, {}
 
         def load_x(n):
             x_rows = sbuf.tile([P, HALVES, I_BATCH], BF16, bufs=2)
@@ -125,18 +128,26 @@ def tile_dartslayer_k_kernel(tc, x, alphas, coeffs, out):
             gate_of[n] = gate
 
         def exponential(n):
-            flat = gate_of[n][:].rearrange("p c j t k -> p (c j t k)")
-            nc.scalar.activation(out=flat, in_=flat, func=ACT.Exp)
+            for c in range(PASSES):
+                flat = gate_of[n][:, c].rearrange("p j t k -> p (j t k)")
+                nc.scalar.activation(out=flat, in_=flat, func=ACT.Exp)
 
         def total(n):
-            sums = sbuf.tile([P, GROUPS], F32)
-            nc.vector.tensor_reduce(
-                out=sums[:],
-                in_=gate_of[n][:].rearrange("p c j t k -> p (c j t) k"),
-                axis=mybir.AxisListType.X,
-                op=ALU.add,
-            )
-            total_of[n] = sums
+            total_of[n] = []
+            for c in range(PASSES):
+                by_group = gate_of[n][:, c].rearrange("p j t k -> p (j t) k")
+                sums_t = psum.tile([P, BLOCKS, P], F32, bufs=2)
+                for q in range(BLOCKS):
+                    for k in range(PRIMS):
+                        nc.tensor.matmul(
+                            out=sums_t[:, q, :],
+                            lhsT=by_group[:, q * P : (q + 1) * P, k],
+                            rhs=identity[:],
+                            is_transpose=True,
+                            start=(k == 0),
+                            stop=(k == PRIMS - 1),
+                        )
+                total_of[n].append(sums_t)
 
         def times_coeffs(n):
             gate = gate_of[n]
@@ -148,23 +159,29 @@ def tile_dartslayer_k_kernel(tc, x, alphas, coeffs, out):
                     op=ALU.mult,
                 )
 
+        def primitives_on_vector(n):
+            x_t = x_t_of[n][:].rearrange("p c b t -> p (c b t)")
+            square = sbuf.tile([P, X_COLS], BF16, align_bytes=64)
+            log_bf = sbuf.tile([P, X_COLS], BF16, align_bytes=64)
+            nc.vector.tensor_tensor(out=square[:], in0=x_t, in1=x_t, op=ALU.mult)
+            nc.vector.tensor_copy(out=log_bf[:], in_=ln_x_of[n][:])
+            prim_of[n] = {1: x_t, 2: square[:], 5: log_bf[:]}
+
         def primitives_exp_set(n):
             x_t = x_t_of[n][:].rearrange("p c b t -> p (c b t)")
             ln_x = ln_x_of[n]
-            square = sbuf.tile([P, X_COLS], BF16, align_bytes=64)
             cube = sbuf.tile([P, X_COLS], BF16, align_bytes=64)
             exp_x = sbuf.tile([P, X_COLS], BF16, align_bytes=64)
-            log_bf = sbuf.tile([P, X_COLS], BF16, align_bytes=64)
             inverse = sbuf.tile([P, X_COLS], BF16, align_bytes=64)
             folded = sbuf.tile([P, X_COLS], F32)
-            nc.scalar.copy(out=log_bf[:], in_=ln_x[:])
             nc.scalar.activation(out=inverse[:], in_=ln_x[:], func=ACT.Exp, scale=-1.0)
             nc.scalar.activation(out=cube[:], in_=ln_x[:], func=ACT.Exp, scale=3.0)
             nc.scalar.activation(out=exp_x[:], in_=x_t, func=ACT.Exp)
-            nc.scalar.activation(out=square[:], in_=x_t, func=ACT.Square)
             nc.scalar.activation(out=folded[:], in_=x_t, func=ACT.Abs, bias=fold_shift[:, 0:1])
             nc.scalar.activation(out=folded[:], in_=folded[:], func=ACT.Abs, bias=fold_shift[:, 1:2])
-            prim_of[n] = [x_t, square[:], cube[:], exp_x[:], log_bf[:], inverse[:]]
+            prim_of[n][3] = cube[:]
+            prim_of[n][4] = exp_x[:]
+            prim_of[n][6] = inverse[:]
             folded_of[n] = folded
 
         def primitive_sin(n):
@@ -172,13 +189,23 @@ def tile_dartslayer_k_kernel(tc, x, alphas, coeffs, out):
             nc.scalar.activation(
                 out=sine[:], in_=folded_of[n][:], func=ACT.Sin, bias=fold_shift[:, 2:3]
             )
-            prim_of[n].append(sine[:])
+            prim_of[n][7] = sine[:]
 
         def log_total(n):
-            nc.scalar.activation(out=total_of[n][:], in_=total_of[n][:], func=ACT.Ln)
+            recip_t = sbuf.tile([P, PASSES, BLOCKS, P], F32)
+            for c in range(PASSES):
+                nc.scalar.activation(out=recip_t[:, c], in_=total_of[n][c][:], func=ACT.Ln)
+            recip_t_of[n] = recip_t
 
         def reciprocal_total(n):
-            nc.scalar.activation(out=total_of[n][:], in_=total_of[n][:], func=ACT.Exp, scale=-1.0)
+            flat = recip_t_of[n][:].rearrange("p c q g -> p (c q g)")
+            nc.scalar.activation(out=flat, in_=flat, func=ACT.Exp, scale=-1.0)
+            recip_of[n] = []
+            for c in range(PASSES):
+                recip = psum.tile([P, BLOCKS, P], F32, bufs=2)
+                for q in range(BLOCKS):
+                    nc.tensor.transpose(recip[:, q, :], recip_t_of[n][:, c, q, :], identity[:])
+                recip_of[n].append(recip)
 
         def quantise_x(n):
             p_codes = sbuf.tile([P, CHANNELS, PASSES, B], U32, align_bytes=64)
@@ -187,27 +214,29 @@ def tile_dartslayer_k_kernel(tc, x, alphas, coeffs, out):
                 nc.vector.quantize_mx(
                     out=p_codes[:, ch].rearrange("p c b -> p (c b)").bitcast(FP8X4),
                     scales=p_scales[:, ch].rearrange("p c b -> p (c b)"),
-                    in_=prim_of[n][ch],
+                    in_=prim_of[n][ch + 1],
                 )
             p_mx_of[n] = (p_codes, p_scales)
 
         def normalise(n):
-            by_group = gate_of[n][:].rearrange("p c j t k -> p (c j t) k")
-            w = sbuf.tile([P, CHANNELS, GROUPS], BF16, align_bytes=64)
-            for k_lo, k_hi in ((1, 4), (4, 8)):
-                nc.vector.tensor_tensor(
-                    out=w[:, k_lo - 1 : k_hi - 1, :].rearrange("p k g -> p g k"),
-                    in0=by_group[:, :, k_lo:k_hi],
-                    in1=total_of[n][:].unsqueeze(2).to_broadcast([P, GROUPS, k_hi - k_lo]),
-                    op=ALU.mult,
-                )
+            w = sbuf.tile([P, CHANNELS, PASSES, PASS_GROUPS], BF16, align_bytes=64)
+            for c in range(PASSES):
+                by_group = gate_of[n][:, c].rearrange("p j t k -> p (j t) k")
+                recip = recip_of[n][c][:].rearrange("p q g -> p (q g)").unsqueeze(2)
+                for k_lo, k_hi in ((1, 4), (4, 8)):
+                    nc.vector.tensor_tensor(
+                        out=w[:, k_lo - 1 : k_hi - 1, c, :].rearrange("p k g -> p g k"),
+                        in0=by_group[:, :, k_lo:k_hi],
+                        in1=recip.to_broadcast([P, PASS_GROUPS, k_hi - k_lo]),
+                        op=ALU.mult,
+                    )
             w_codes = sbuf.tile([P, CHANNELS, PASSES, J], U32, align_bytes=64)
             w_scales = sbuf.tile([P, CHANNELS, PASSES, J], U8, align_bytes=64)
             for ch in range(CHANNELS):
                 nc.vector.quantize_mx(
                     out=w_codes[:, ch].rearrange("p c j -> p (c j)").bitcast(FP8X4),
                     scales=w_scales[:, ch].rearrange("p c j -> p (c j)"),
-                    in_=w[:, ch, :],
+                    in_=w[:, ch].rearrange("p c g -> p (c g)"),
                 )
             w_mx_of[n] = (w_codes, w_scales)
 
@@ -243,12 +272,14 @@ def tile_dartslayer_k_kernel(tc, x, alphas, coeffs, out):
                 if n > 0:
                     reciprocal_total(n - 1)
                     normalise(n - 1)
-                    multiply(n - 1)
                 exponential(n)
                 total(n)
+                if n > 0:
+                    multiply(n - 1)
                 times_coeffs(n)
                 if n + 1 < BATCHES:
                     load_weights(n + 1, coeffs, coeff_of, "coeff_rows")
+                primitives_on_vector(n)
                 primitives_exp_set(n)
                 primitive_sin(n)
                 if n + 1 < BATCHES:

@@ -153,9 +153,9 @@ def tile_dartslayer_k_kernel(tc, x, alphas, coeffs, out):
             gate = gate_of[n]
             for c in range(PASSES):
                 nc.vector.tensor_tensor(
-                    out=gate[:, c, :, :, 1:PRIMS],
-                    in0=gate[:, c, :, :, 1:PRIMS],
-                    in1=coeff_of[n][:, c].rearrange("p t j k -> p j t k")[:, :, :, 1:PRIMS],
+                    out=gate[:, c],
+                    in0=gate[:, c],
+                    in1=coeff_of[n][:, c].rearrange("p t j k -> p j t k"),
                     op=ALU.mult,
                 )
 

@@ -21,10 +21,9 @@ PASSES = 2
 I_BATCH = PASSES * K_PASS
 BATCHES = I // I_BATCH
 HALVES = B // P
-GROUPS = PASSES * J * PACK
 X_COLS = PASSES * B * PACK
-PASS_GROUPS = J * PACK
-BLOCKS = PASS_GROUPS // P
+GROUPS = J * PACK
+BLOCKS = GROUPS // P
 
 FLOPS = 2 * B * J * I * CHANNELS
 
@@ -55,26 +54,34 @@ def tile_dartslayer_k_kernel(tc, x, alphas, coeffs, out):
         recip_t_of, recip_of = {}, {}
 
         def load_x(n):
-            x_rows = sbuf.tile([P, HALVES, I_BATCH], BF16, bufs=2)
+            x_rows = sbuf.tile([P, HALVES, I_BATCH], BF16)
             nc.sync.dma_start(
                 out=x_rows[:],
                 in_=x[:, n * I_BATCH : (n + 1) * I_BATCH].rearrange("(h b) i -> b h i", h=HALVES),
             )
             x_rows_of[n] = x_rows
 
-        def load_weights(n, source, tiles, label):
-            rows = sbuf.tile([P, PASSES, PACK, J, PRIMS], BF16, name=label)
-            nc.sync.dma_start(
-                out=rows[:].rearrange("p c t j k -> p c (t j k)"),
-                in_=source[n * I_BATCH : (n + 1) * I_BATCH].rearrange(
-                    "(c p t) j k -> p c (t j k)", c=PASSES, p=P, t=PACK
-                ),
-            )
+        def load_weights(n, source, tiles, label, copies):
+            rows = sbuf.tile([P, PASSES, PACK, J, PRIMS], BF16, name=label, bufs=copies)
+            for c in range(PASSES):
+                first_row = (n * PASSES + c) * K_PASS
+                nc.sync.dma_start(
+                    out=rows[:, c].rearrange("p t j k -> p (t j k)"),
+                    in_=source[first_row : first_row + K_PASS].rearrange(
+                        "(p t) j k -> p (t j k)", p=P, t=PACK
+                    ),
+                )
             tiles[n] = rows
+
+        def load_alphas(n):
+            load_weights(n, alphas, alpha_of, "alpha_rows", 2)
+
+        def load_coeffs(n):
+            load_weights(n, coeffs, coeff_of, "coeff_rows", 1)
 
         def transpose_x(n):
             words = x_rows_of[n][:].bitcast(F32)
-            x_t = sbuf.tile([P, PASSES, B, PACK], BF16, bufs=2, align_bytes=64)
+            x_t = sbuf.tile([P, PASSES, B, PACK], BF16, bufs=3, align_bytes=64)
             x_t_words = x_t[:].bitcast(F32)
             pass_words = K_PASS // 2
             for c in range(PASSES):
@@ -90,39 +97,43 @@ def tile_dartslayer_k_kernel(tc, x, alphas, coeffs, out):
                     out=x_t_words[:, c].rearrange("p (h b) u -> p h b u", h=HALVES),
                     in_=turned[:].rearrange("p h u b -> p h b u"),
                 )
-            x_t_of[n] = x_t
+            x_t_of[n] = x_t[:].rearrange("p c b t -> p (c b t)")
+            prim_of[n] = {1: x_t_of[n]}
 
         def log_x(n):
             ln_x = sbuf.tile([P, X_COLS], F32)
-            nc.scalar.activation(
-                out=ln_x[:], in_=x_t_of[n][:].rearrange("p c b t -> p (c b t)"), func=ACT.Ln
-            )
+            nc.scalar.activation(out=ln_x[:], in_=x_t_of[n], func=ACT.Ln)
             ln_x_of[n] = ln_x
 
         def shift(n):
             rows = alpha_of[n]
-            by_group = rows[:].rearrange("p c t j k -> p (c t j) k")
-            max4 = sbuf.tile([P, GROUPS, 4], BF16)
-            max2 = sbuf.tile([P, GROUPS, 2], BF16)
+            max4 = sbuf.tile([P, PASSES, GROUPS, 4], BF16)
+            max2 = sbuf.tile([P, PASSES, GROUPS, 2], BF16)
             max1 = sbuf.tile([P, PASSES, PACK, J, 1], BF16)
-            nc.vector.tensor_tensor(
-                out=max4[:], in0=by_group[:, :, 0:4], in1=by_group[:, :, 4:8], op=ALU.max
-            )
-            nc.vector.tensor_tensor(
-                out=max2[:], in0=max4[:, :, 0:2], in1=max4[:, :, 2:4], op=ALU.max
-            )
-            nc.vector.tensor_tensor(
-                out=max1[:].rearrange("p c t j o -> p (c t j) o"),
-                in0=max2[:, :, 0:1],
-                in1=max2[:, :, 1:2],
-                op=ALU.max,
-            )
             gate = sbuf.tile([P, PASSES, J, PACK, PRIMS], F32, bufs=2)
+            for c in range(PASSES):
+                by_group = rows[:, c].rearrange("p t j k -> p (t j) k")
+                nc.vector.tensor_tensor(
+                    out=max4[:, c], in0=by_group[:, :, 0:4], in1=by_group[:, :, 4:8], op=ALU.max
+                )
+            for c in range(PASSES):
+                nc.vector.tensor_tensor(
+                    out=max2[:, c], in0=max4[:, c, :, 0:2], in1=max4[:, c, :, 2:4], op=ALU.max
+                )
+            for c in range(PASSES):
+                nc.vector.tensor_tensor(
+                    out=max1[:, c].rearrange("p t j o -> p (t j) o"),
+                    in0=max2[:, c, :, 0:1],
+                    in1=max2[:, c, :, 1:2],
+                    op=ALU.max,
+                )
             for c in range(PASSES):
                 nc.vector.tensor_tensor(
                     out=gate[:, c],
                     in0=rows[:, c].rearrange("p t j k -> p j t k"),
-                    in1=max1[:, c].rearrange("p t j o -> p j t o").to_broadcast([P, J, PACK, PRIMS]),
+                    in1=max1[:, c]
+                    .rearrange("p t j o -> p j t o")
+                    .to_broadcast([P, J, PACK, PRIMS]),
                     op=ALU.subtract,
                 )
             gate_of[n] = gate
@@ -159,33 +170,38 @@ def tile_dartslayer_k_kernel(tc, x, alphas, coeffs, out):
                     op=ALU.mult,
                 )
 
-        def primitives_on_vector(n):
-            x_t = x_t_of[n][:].rearrange("p c b t -> p (c b t)")
-            square = sbuf.tile([P, X_COLS], BF16, align_bytes=64)
+        def primitive_log(n):
             log_bf = sbuf.tile([P, X_COLS], BF16, align_bytes=64)
-            nc.vector.tensor_tensor(out=square[:], in0=x_t, in1=x_t, op=ALU.mult)
             nc.vector.tensor_copy(out=log_bf[:], in_=ln_x_of[n][:])
-            prim_of[n] = {1: x_t, 2: square[:], 5: log_bf[:]}
+            prim_of[n][5] = log_bf[:]
 
         def primitives_exp_set(n):
-            x_t = x_t_of[n][:].rearrange("p c b t -> p (c b t)")
             ln_x = ln_x_of[n]
+            square = sbuf.tile([P, X_COLS], BF16, align_bytes=64)
             cube = sbuf.tile([P, X_COLS], BF16, align_bytes=64)
             exp_x = sbuf.tile([P, X_COLS], BF16, align_bytes=64)
             inverse = sbuf.tile([P, X_COLS], BF16, align_bytes=64)
-            folded = sbuf.tile([P, X_COLS], F32)
             nc.scalar.activation(out=inverse[:], in_=ln_x[:], func=ACT.Exp, scale=-1.0)
             nc.scalar.activation(out=cube[:], in_=ln_x[:], func=ACT.Exp, scale=3.0)
-            nc.scalar.activation(out=exp_x[:], in_=x_t, func=ACT.Exp)
-            nc.scalar.activation(out=folded[:], in_=x_t, func=ACT.Abs, bias=fold_shift[:, 0:1])
-            nc.scalar.activation(out=folded[:], in_=folded[:], func=ACT.Abs, bias=fold_shift[:, 1:2])
+            nc.scalar.activation(out=exp_x[:], in_=x_t_of[n], func=ACT.Exp)
+            nc.scalar.activation(out=square[:], in_=x_t_of[n], func=ACT.Square)
+            prim_of[n][2] = square[:]
             prim_of[n][3] = cube[:]
             prim_of[n][4] = exp_x[:]
             prim_of[n][6] = inverse[:]
+
+        def fold_x(n):
+            folded = sbuf.tile([P, X_COLS], F32)
+            nc.scalar.activation(
+                out=folded[:], in_=x_t_of[n], func=ACT.Abs, bias=fold_shift[:, 0:1]
+            )
+            nc.scalar.activation(
+                out=folded[:], in_=folded[:], func=ACT.Abs, bias=fold_shift[:, 1:2]
+            )
             folded_of[n] = folded
 
         def primitive_sin(n):
-            sine = sbuf.tile([P, X_COLS], BF16, align_bytes=64)
+            sine = sbuf.tile([P, X_COLS], BF16, bufs=2, align_bytes=64)
             nc.scalar.activation(
                 out=sine[:], in_=folded_of[n][:], func=ACT.Sin, bias=fold_shift[:, 2:3]
             )
@@ -219,7 +235,7 @@ def tile_dartslayer_k_kernel(tc, x, alphas, coeffs, out):
             p_mx_of[n] = (p_codes, p_scales)
 
         def normalise(n):
-            w = sbuf.tile([P, CHANNELS, PASSES, PASS_GROUPS], BF16, align_bytes=64)
+            w = sbuf.tile([P, CHANNELS, PASSES, GROUPS], BF16, align_bytes=64)
             for c in range(PASSES):
                 by_group = gate_of[n][:, c].rearrange("p j t k -> p (j t) k")
                 recip = recip_of[n][c][:].rearrange("p q g -> p (q g)").unsqueeze(2)
@@ -227,7 +243,7 @@ def tile_dartslayer_k_kernel(tc, x, alphas, coeffs, out):
                     nc.vector.tensor_tensor(
                         out=w[:, k_lo - 1 : k_hi - 1, c, :].rearrange("p k g -> p g k"),
                         in0=by_group[:, :, k_lo:k_hi],
-                        in1=recip.to_broadcast([P, PASS_GROUPS, k_hi - k_lo]),
+                        in1=recip.to_broadcast([P, GROUPS, k_hi - k_lo]),
                         op=ALU.mult,
                     )
             w_codes = sbuf.tile([P, CHANNELS, PASSES, J], U32, align_bytes=64)
@@ -259,43 +275,32 @@ def tile_dartslayer_k_kernel(tc, x, alphas, coeffs, out):
                             stop=last,
                         )
 
+        def run(stage, n):
+            if 0 <= n < BATCHES:
+                stage(n)
+
         with tc.manual_schedule():
             load_x(0)
-            load_weights(0, alphas, alpha_of, "alpha_rows")
-            load_weights(0, coeffs, coeff_of, "coeff_rows")
-            load_x(1)
-            transpose_x(0)
-            log_x(0)
-            shift(0)
-            load_weights(1, alphas, alpha_of, "alpha_rows")
-            for n in range(BATCHES):
-                if n > 0:
-                    reciprocal_total(n - 1)
-                    normalise(n - 1)
-                exponential(n)
-                total(n)
-                if n > 0:
-                    multiply(n - 1)
-                times_coeffs(n)
-                if n + 1 < BATCHES:
-                    load_weights(n + 1, coeffs, coeff_of, "coeff_rows")
-                primitives_on_vector(n)
-                primitives_exp_set(n)
-                primitive_sin(n)
-                if n + 1 < BATCHES:
-                    shift(n + 1)
-                if n + 2 < BATCHES:
-                    load_weights(n + 2, alphas, alpha_of, "alpha_rows")
-                log_total(n)
-                if n + 1 < BATCHES:
-                    transpose_x(n + 1)
-                    log_x(n + 1)
-                if n + 2 < BATCHES:
-                    load_x(n + 2)
-                quantise_x(n)
-            reciprocal_total(BATCHES - 1)
-            normalise(BATCHES - 1)
-            multiply(BATCHES - 1)
+            load_alphas(0)
+            for n in range(-2, BATCHES + 1):
+                run(reciprocal_total, n - 1)
+                run(normalise, n - 1)
+                run(primitive_log, n)
+                run(shift, n + 1)
+                run(load_alphas, n + 3)
+                run(exponential, n)
+                run(total, n)
+                run(multiply, n - 1)
+                run(times_coeffs, n)
+                run(load_coeffs, n + 1)
+                run(primitives_exp_set, n)
+                run(fold_x, n + 1)
+                run(primitive_sin, n + 1)
+                run(log_total, n)
+                run(transpose_x, n + 2)
+                run(load_x, n + 3)
+                run(log_x, n + 1)
+                run(quantise_x, n)
             for h in range(HALVES):
                 result = sbuf.tile([P, J], F32, bufs=2)
                 nc.vector.tensor_copy(out=result[:], in_=acc[h][:])

@@ -170,22 +170,28 @@ def tile_dartslayer_k_kernel(tc, x, alphas, coeffs, out):
                     op=ALU.mult,
                 )
 
-        def primitive_log(n):
-            log_bf = sbuf.tile([P, X_COLS], BF16, align_bytes=64)
-            nc.vector.tensor_copy(out=log_bf[:], in_=ln_x_of[n][:])
-            prim_of[n][5] = log_bf[:]
+        def primitives_on_gpsimd(n):
+            log_bf = sbuf.tile([P, PASSES, B * PACK], BF16, align_bytes=64)
+            square = sbuf.tile([P, PASSES, B * PACK], BF16, align_bytes=64)
+            ln_x = ln_x_of[n][:].rearrange("p (c v) -> p c v", c=PASSES)
+            x_t = x_t_of[n].rearrange("p (c v) -> p c v", c=PASSES)
+            for c in range(PASSES):
+                nc.gpsimd.tensor_scalar(
+                    out=log_bf[:, c], in0=ln_x[:, c], scalar1=1.0, scalar2=0.0, op0=ALU.mult, op1=ALU.add
+                )
+            for c in range(PASSES):
+                nc.gpsimd.tensor_tensor(out=square[:, c], in0=x_t[:, c], in1=x_t[:, c], op=ALU.mult)
+            prim_of[n][2] = square[:].rearrange("p c v -> p (c v)")
+            prim_of[n][5] = log_bf[:].rearrange("p c v -> p (c v)")
 
         def primitives_exp_set(n):
             ln_x = ln_x_of[n]
-            square = sbuf.tile([P, X_COLS], BF16, align_bytes=64)
             cube = sbuf.tile([P, X_COLS], BF16, align_bytes=64)
             exp_x = sbuf.tile([P, X_COLS], BF16, align_bytes=64)
             inverse = sbuf.tile([P, X_COLS], BF16, align_bytes=64)
             nc.scalar.activation(out=inverse[:], in_=ln_x[:], func=ACT.Exp, scale=-1.0)
             nc.scalar.activation(out=cube[:], in_=ln_x[:], func=ACT.Exp, scale=3.0)
             nc.scalar.activation(out=exp_x[:], in_=x_t_of[n], func=ACT.Exp)
-            nc.scalar.activation(out=square[:], in_=x_t_of[n], func=ACT.Square)
-            prim_of[n][2] = square[:]
             prim_of[n][3] = cube[:]
             prim_of[n][4] = exp_x[:]
             prim_of[n][6] = inverse[:]
@@ -285,7 +291,7 @@ def tile_dartslayer_k_kernel(tc, x, alphas, coeffs, out):
             for n in range(-2, BATCHES + 1):
                 run(reciprocal_total, n - 1)
                 run(normalise, n - 1)
-                run(primitive_log, n)
+                run(primitives_on_gpsimd, n)
                 run(shift, n + 1)
                 run(load_alphas, n + 3)
                 run(exponential, n)

@@ -23,6 +23,7 @@ BATCHES = I // I_BATCH
 HALVES = B // P
 X_COLS = PASSES * B * PACK
 GROUPS = J * PACK
+SAFE = 16.0
 BLOCKS = GROUPS // P
 
 FLOPS = 2 * B * J * I * CHANNELS
@@ -109,12 +110,11 @@ def tile_dartslayer_k_kernel(tc, x, alphas, coeffs, out):
             rows = alpha_of[n]
             max4 = sbuf.tile([P, PASSES, GROUPS, 4], BF16)
             max2 = sbuf.tile([P, PASSES, GROUPS, 2], BF16)
-            max1 = sbuf.tile([P, PASSES, PACK, J, 1], BF16)
-            gate = sbuf.tile([P, PASSES, J, PACK, PRIMS], F32, bufs=2)
+            max1 = sbuf.tile([P, PASSES, GROUPS, 2], BF16)
+            by_group = [rows[:, c].rearrange("p t j k -> p (t j) k") for c in range(PASSES)]
             for c in range(PASSES):
-                by_group = rows[:, c].rearrange("p t j k -> p (t j) k")
                 nc.vector.tensor_tensor(
-                    out=max4[:, c], in0=by_group[:, :, 0:4], in1=by_group[:, :, 4:8], op=ALU.max
+                    out=max4[:, c], in0=by_group[c][:, :, 0:4], in1=by_group[c][:, :, 4:8], op=ALU.max
                 )
             for c in range(PASSES):
                 nc.vector.tensor_tensor(
@@ -122,26 +122,33 @@ def tile_dartslayer_k_kernel(tc, x, alphas, coeffs, out):
                 )
             for c in range(PASSES):
                 nc.vector.tensor_tensor(
-                    out=max1[:, c].rearrange("p t j o -> p (t j) o"),
-                    in0=max2[:, c, :, 0:1],
-                    in1=max2[:, c, :, 1:2],
-                    op=ALU.max,
+                    out=max1[:, c], in0=max2[:, c], in1=max2[:, c, :, ::-1], op=ALU.max
+                )
+            for c in range(PASSES):
+                nc.vector.tensor_scalar(
+                    out=max2[:, c], in0=max1[:, c], scalar1=-SAFE, scalar2=SAFE, op0=ALU.max, op1=ALU.min
                 )
             for c in range(PASSES):
                 nc.vector.tensor_tensor(
-                    out=gate[:, c],
-                    in0=rows[:, c].rearrange("p t j k -> p j t k"),
-                    in1=max1[:, c]
-                    .rearrange("p t j o -> p j t o")
-                    .to_broadcast([P, J, PACK, PRIMS]),
+                    out=max1[:, c], in0=max1[:, c], in1=max2[:, c], op=ALU.subtract
+                )
+            for c in range(PASSES):
+                nc.vector.tensor_tensor(
+                    out=by_group[c].rearrange("p g (h u) -> p g h u", u=2),
+                    in0=by_group[c].rearrange("p g (h u) -> p g h u", u=2),
+                    in1=max1[:, c].unsqueeze(2).to_broadcast([P, GROUPS, PRIMS // 2, 2]),
                     op=ALU.subtract,
                 )
-            gate_of[n] = gate
 
         def exponential(n):
+            gate = sbuf.tile([P, PASSES, J, PACK, PRIMS], F32, bufs=2)
             for c in range(PASSES):
-                flat = gate_of[n][:, c].rearrange("p j t k -> p (j t k)")
-                nc.scalar.activation(out=flat, in_=flat, func=ACT.Exp)
+                nc.scalar.activation(
+                    out=gate[:, c],
+                    in_=alpha_of[n][:, c].rearrange("p t j k -> p j t k"),
+                    func=ACT.Exp,
+                )
+            gate_of[n] = gate
 
         def total(n):
             total_of[n] = []
@@ -287,14 +294,13 @@ def tile_dartslayer_k_kernel(tc, x, alphas, coeffs, out):
 
         with tc.manual_schedule():
             load_x(0)
-            load_alphas(0)
             for n in range(-2, BATCHES + 1):
                 run(reciprocal_total, n - 1)
                 run(normalise, n - 1)
                 run(primitives_on_gpsimd, n)
                 run(shift, n + 1)
-                run(load_alphas, n + 3)
                 run(exponential, n)
+                run(load_alphas, n + 2)
                 run(total, n)
                 run(multiply, n - 1)
                 run(times_coeffs, n)

@@ -24,7 +24,6 @@ HALVES = B // P
 X_COLS = PASSES * B * PACK
 GROUPS = J * PACK
 SAFE = 16.0
-BLOCKS = GROUPS // P
 
 FLOPS = 2 * B * J * I * CHANNELS
 
@@ -52,7 +51,7 @@ def tile_dartslayer_k_kernel(tc, x, alphas, coeffs, out):
 
         x_rows_of, x_t_of, ln_x_of, alpha_of, coeff_of = {}, {}, {}, {}, {}
         gate_of, total_of, prim_of, folded_of, p_mx_of, w_mx_of = {}, {}, {}, {}, {}, {}
-        recip_t_of, recip_of = {}, {}
+        recip_t_of, recip_of, w_of = {}, {}, {}
 
         def load_x(n):
             x_rows = sbuf.tile([P, HALVES, I_BATCH], BF16)
@@ -82,7 +81,7 @@ def tile_dartslayer_k_kernel(tc, x, alphas, coeffs, out):
 
         def transpose_x(n):
             words = x_rows_of[n][:].bitcast(F32)
-            x_t = sbuf.tile([P, PASSES, B, PACK], BF16, bufs=3, align_bytes=64)
+            x_t = sbuf.tile([P, PASSES, B, PACK], BF16, bufs=2, align_bytes=64)
             x_t_words = x_t[:].bitcast(F32)
             pass_words = K_PASS // 2
             for c in range(PASSES):
@@ -110,7 +109,10 @@ def tile_dartslayer_k_kernel(tc, x, alphas, coeffs, out):
             rows = alpha_of[n]
             max4 = sbuf.tile([P, PASSES, GROUPS, 4], BF16)
             max2 = sbuf.tile([P, PASSES, GROUPS, 2], BF16)
-            max1 = sbuf.tile([P, PASSES, GROUPS, 2], BF16)
+            max1 = [
+                max4[:, c].rearrange("p g k -> p (g k)")[:, : GROUPS * 2].rearrange("p (g u) -> p g u", u=2)
+                for c in range(PASSES)
+            ]
             by_group = [rows[:, c].rearrange("p t j k -> p (t j) k") for c in range(PASSES)]
             for c in range(PASSES):
                 nc.vector.tensor_tensor(
@@ -122,29 +124,29 @@ def tile_dartslayer_k_kernel(tc, x, alphas, coeffs, out):
                 )
             for c in range(PASSES):
                 nc.vector.tensor_tensor(
-                    out=max1[:, c], in0=max2[:, c], in1=max2[:, c, :, ::-1], op=ALU.max
+                    out=max1[c], in0=max2[:, c], in1=max2[:, c, :, ::-1], op=ALU.max
                 )
             for c in range(PASSES):
                 nc.vector.tensor_scalar(
-                    out=max2[:, c], in0=max1[:, c], scalar1=-SAFE, scalar2=SAFE, op0=ALU.max, op1=ALU.min
+                    out=max2[:, c], in0=max1[c], scalar1=-SAFE, scalar2=SAFE, op0=ALU.max, op1=ALU.min
                 )
             for c in range(PASSES):
                 nc.vector.tensor_tensor(
-                    out=max1[:, c], in0=max1[:, c], in1=max2[:, c], op=ALU.subtract
+                    out=max1[c], in0=max1[c], in1=max2[:, c], op=ALU.subtract
                 )
             for c in range(PASSES):
                 nc.vector.tensor_tensor(
                     out=by_group[c].rearrange("p g (h u) -> p g h u", u=2),
                     in0=by_group[c].rearrange("p g (h u) -> p g h u", u=2),
-                    in1=max1[:, c].unsqueeze(2).to_broadcast([P, GROUPS, PRIMS // 2, 2]),
+                    in1=max1[c].unsqueeze(2).to_broadcast([P, GROUPS, PRIMS // 2, 2]),
                     op=ALU.subtract,
                 )
 
         def exponential(n):
-            gate = sbuf.tile([P, PASSES, J, PACK, PRIMS], F32, bufs=2)
+            gate = sbuf.tile([P, PASSES, GROUPS * PRIMS], F32, bufs=2)
             for c in range(PASSES):
                 nc.scalar.activation(
-                    out=gate[:, c],
+                    out=gate[:, c].rearrange("p (j t k) -> p j t k", t=PACK, k=PRIMS),
                     in_=alpha_of[n][:, c].rearrange("p t j k -> p j t k"),
                     func=ACT.Exp,
                 )
@@ -153,13 +155,13 @@ def tile_dartslayer_k_kernel(tc, x, alphas, coeffs, out):
         def total(n):
             total_of[n] = []
             for c in range(PASSES):
-                by_group = gate_of[n][:, c].rearrange("p j t k -> p (j t) k")
-                sums_t = psum.tile([P, BLOCKS, P], F32, bufs=2)
-                for q in range(BLOCKS):
+                gate = gate_of[n][:, c].rearrange("p (j t k) -> p j t k", t=PACK, k=PRIMS)
+                sums_t = psum.tile([P, PACK, P], F32, bufs=2)
+                for t in range(PACK):
                     for k in range(PRIMS):
                         nc.tensor.matmul(
-                            out=sums_t[:, q, :],
-                            lhsT=by_group[:, q * P : (q + 1) * P, k],
+                            out=sums_t[:, t, :],
+                            lhsT=gate[:, :, t, k],
                             rhs=identity[:],
                             is_transpose=True,
                             start=(k == 0),
@@ -168,12 +170,12 @@ def tile_dartslayer_k_kernel(tc, x, alphas, coeffs, out):
                 total_of[n].append(sums_t)
 
         def times_coeffs(n):
-            gate = gate_of[n]
             for c in range(PASSES):
+                gate = gate_of[n][:, c]
                 nc.vector.tensor_tensor(
-                    out=gate[:, c],
-                    in0=gate[:, c],
-                    in1=coeff_of[n][:, c].rearrange("p t j k -> p j t k"),
+                    out=gate[:, : GROUPS * CHANNELS].rearrange("p (j t k) -> p j t k", t=PACK, k=CHANNELS),
+                    in0=gate.rearrange("p (j t k) -> p j t k", t=PACK, k=PRIMS)[:, :, :, 1:PRIMS],
+                    in1=coeff_of[n][:, c, :, :, 1:PRIMS].rearrange("p t j k -> p j t k"),
                     op=ALU.mult,
                 )
 
@@ -204,7 +206,7 @@ def tile_dartslayer_k_kernel(tc, x, alphas, coeffs, out):
             prim_of[n][6] = inverse[:]
 
         def fold_x(n):
-            folded = sbuf.tile([P, X_COLS], F32)
+            folded = sbuf.tile([P, X_COLS], F32, bufs=2)
             nc.scalar.activation(
                 out=folded[:], in_=x_t_of[n], func=ACT.Abs, bias=fold_shift[:, 0:1]
             )
@@ -221,19 +223,25 @@ def tile_dartslayer_k_kernel(tc, x, alphas, coeffs, out):
             prim_of[n][7] = sine[:]
 
         def log_total(n):
-            recip_t = sbuf.tile([P, PASSES, BLOCKS, P], F32)
+            w = sbuf.tile([P, CHANNELS, PASSES, GROUPS], BF16, align_bytes=64)
+            recip_t = w[:, CHANNELS - 2 :].rearrange("p k c g -> p (k c g)").bitcast(F32)
+            recip_t_of[n] = recip_t.rearrange("p (c g) -> p c g", c=PASSES)
+            w_of[n] = w
             for c in range(PASSES):
-                nc.scalar.activation(out=recip_t[:, c], in_=total_of[n][c][:], func=ACT.Ln)
-            recip_t_of[n] = recip_t
+                nc.scalar.activation(
+                    out=recip_t_of[n][:, c],
+                    in_=total_of[n][c][:].rearrange("p t j -> p (t j)"),
+                    func=ACT.Ln,
+                )
 
         def reciprocal_total(n):
-            flat = recip_t_of[n][:].rearrange("p c q g -> p (c q g)")
-            nc.scalar.activation(out=flat, in_=flat, func=ACT.Exp, scale=-1.0)
+            recip_t = recip_t_of[n]
+            nc.scalar.activation(out=recip_t, in_=recip_t, func=ACT.Exp, scale=-1.0)
             recip_of[n] = []
             for c in range(PASSES):
-                recip = psum.tile([P, BLOCKS, P], F32, bufs=2)
-                for q in range(BLOCKS):
-                    nc.tensor.transpose(recip[:, q, :], recip_t_of[n][:, c, q, :], identity[:])
+                recip = psum.tile([P, PACK, P], F32, bufs=2)
+                for t in range(PACK):
+                    nc.tensor.transpose(recip[:, t, :], recip_t[:, c, t * P : (t + 1) * P], identity[:])
                 recip_of[n].append(recip)
 
         def quantise_x(n):
@@ -248,15 +256,17 @@ def tile_dartslayer_k_kernel(tc, x, alphas, coeffs, out):
             p_mx_of[n] = (p_codes, p_scales)
 
         def normalise(n):
-            w = sbuf.tile([P, CHANNELS, PASSES, GROUPS], BF16, align_bytes=64)
+            w = w_of[n]
             for c in range(PASSES):
-                by_group = gate_of[n][:, c].rearrange("p j t k -> p (j t) k")
-                recip = recip_of[n][c][:].rearrange("p q g -> p (q g)").unsqueeze(2)
-                for k_lo, k_hi in ((1, 4), (4, 8)):
+                product = gate_of[n][:, c, : GROUPS * CHANNELS].rearrange(
+                    "p (j t k) -> p j t k", t=PACK, k=CHANNELS
+                )
+                recip = recip_of[n][c][:].rearrange("p t j -> p j t").unsqueeze(3)
+                for k_lo, k_hi in ((0, 3), (3, 7)):
                     nc.vector.tensor_tensor(
-                        out=w[:, k_lo - 1 : k_hi - 1, c, :].rearrange("p k g -> p g k"),
-                        in0=by_group[:, :, k_lo:k_hi],
-                        in1=recip.to_broadcast([P, GROUPS, k_hi - k_lo]),
+                        out=w[:, k_lo:k_hi, c, :].rearrange("p k (j t) -> p j t k", t=PACK),
+                        in0=product[:, :, :, k_lo:k_hi],
+                        in1=recip.to_broadcast([P, J, PACK, k_hi - k_lo]),
                         op=ALU.mult,
                     )
             w_codes = sbuf.tile([P, CHANNELS, PASSES, J], U32, align_bytes=64)
@@ -288,29 +298,34 @@ def tile_dartslayer_k_kernel(tc, x, alphas, coeffs, out):
                             stop=last,
                         )
 
+        folded_in = {0: (), 1: (1, 2)}
+
         def run(stage, n):
             if 0 <= n < BATCHES:
                 stage(n)
 
         with tc.manual_schedule():
             load_x(0)
-            for n in range(-2, BATCHES + 1):
+            load_alphas(0)
+            for n in range(-1, BATCHES + 1):
                 run(reciprocal_total, n - 1)
                 run(normalise, n - 1)
                 run(primitives_on_gpsimd, n)
                 run(shift, n + 1)
                 run(exponential, n)
                 run(load_alphas, n + 2)
+                run(transpose_x, n + 1)
+                run(load_x, n + 2)
                 run(total, n)
                 run(multiply, n - 1)
                 run(times_coeffs, n)
                 run(load_coeffs, n + 1)
                 run(primitives_exp_set, n)
-                run(fold_x, n + 1)
-                run(primitive_sin, n + 1)
+                for m in folded_in.get(n, (n + 1,)):
+                    run(fold_x, m)
+                for m in (0,) if n == -1 else (n, n + 1) if n % 2 == 1 else ():
+                    run(primitive_sin, m)
                 run(log_total, n)
-                run(transpose_x, n + 2)
-                run(load_x, n + 3)
                 run(log_x, n + 1)
                 run(quantise_x, n)
             for h in range(HALVES):

@@ -23,6 +23,7 @@ BATCHES = I // I_BATCH
 HALVES = B // P
 X_COLS = PASSES * B * PACK
 GROUPS = J * PACK
+SHARES = ((("vector", 0, J),), (("vector", 0, 48), ("gpsimd", 48, J)))
 SAFE = 16.0
 
 FLOPS = 2 * B * J * I * CHANNELS
@@ -38,8 +39,8 @@ def tile_dartslayer_k_kernel(tc, x, alphas, coeffs, out):
         make_identity(nc, identity[:])
         zero = sbuf.tile([P, 1], F32)
         nc.vector.memset(zero[:], 0.0)
-        fold_shift = sbuf.tile([P, 3], F32)
-        for place, turns in enumerate((2.5, 1.0, 0.5)):
+        fold_shift = sbuf.tile([P, 4], F32)
+        for place, turns in enumerate((2.5, 1.0, 0.5, 2.0)):
             nc.vector.tensor_scalar_add(
                 out=fold_shift[:, place : place + 1], in0=zero[:], scalar1=-turns * math.pi
             )
@@ -51,7 +52,7 @@ def tile_dartslayer_k_kernel(tc, x, alphas, coeffs, out):
 
         x_rows_of, x_t_of, ln_x_of, alpha_of, coeff_of = {}, {}, {}, {}, {}
         gate_of, total_of, prim_of, folded_of, p_mx_of, w_mx_of = {}, {}, {}, {}, {}, {}
-        recip_t_of, recip_of, w_of = {}, {}, {}
+        recip_t_of, recip_of, w_of, scratch_of = {}, {}, {}, {}
 
         def load_x(n):
             x_rows = sbuf.tile([P, HALVES, I_BATCH], BF16)
@@ -105,9 +106,15 @@ def tile_dartslayer_k_kernel(tc, x, alphas, coeffs, out):
             nc.scalar.activation(out=ln_x[:], in_=x_t_of[n], func=ACT.Ln)
             ln_x_of[n] = ln_x
 
+        def new_scratch(n):
+            scratch = sbuf.tile([P, PASSES * GROUPS * 4], BF16, align_bytes=64)
+            scratch_of[n] = scratch
+            return scratch
+
         def shift(n):
             rows = alpha_of[n]
-            max4 = sbuf.tile([P, PASSES, GROUPS, 4], BF16)
+            scratch = new_scratch(n)
+            max4 = scratch[:].rearrange("p (c g k) -> p c g k", c=PASSES, k=4)
             max2 = sbuf.tile([P, PASSES, GROUPS, 2], BF16)
             max1 = [
                 max4[:, c].rearrange("p g k -> p (g k)")[:, : GROUPS * 2].rearrange("p (g u) -> p g u", u=2)
@@ -169,29 +176,41 @@ def tile_dartslayer_k_kernel(tc, x, alphas, coeffs, out):
                         )
                 total_of[n].append(sums_t)
 
-        def times_coeffs(n):
-            for c in range(PASSES):
-                gate = gate_of[n][:, c]
-                nc.vector.tensor_tensor(
-                    out=gate[:, : GROUPS * CHANNELS].rearrange("p (j t k) -> p j t k", t=PACK, k=CHANNELS),
-                    in0=gate.rearrange("p (j t k) -> p j t k", t=PACK, k=PRIMS)[:, :, :, 1:PRIMS],
-                    in1=coeff_of[n][:, c, :, :, 1:PRIMS].rearrange("p t j k -> p j t k"),
-                    op=ALU.mult,
-                )
+        def products(n, c, j_lo, j_hi):
+            first = j_lo * PACK * PRIMS
+            size = (j_hi - j_lo) * PACK * CHANNELS
+            return gate_of[n][:, c, first : first + size].rearrange(
+                "p (j t k) -> p j t k", t=PACK, k=CHANNELS
+            )
 
-        def primitives_on_gpsimd(n):
-            log_bf = sbuf.tile([P, PASSES, B * PACK], BF16, align_bytes=64)
-            square = sbuf.tile([P, PASSES, B * PACK], BF16, align_bytes=64)
-            ln_x = ln_x_of[n][:].rearrange("p (c v) -> p c v", c=PASSES)
-            x_t = x_t_of[n].rearrange("p (c v) -> p c v", c=PASSES)
-            for c in range(PASSES):
-                nc.gpsimd.tensor_scalar(
-                    out=log_bf[:, c], in0=ln_x[:, c], scalar1=1.0, scalar2=0.0, op0=ALU.mult, op1=ALU.add
-                )
-            for c in range(PASSES):
-                nc.gpsimd.tensor_tensor(out=square[:, c], in0=x_t[:, c], in1=x_t[:, c], op=ALU.mult)
-            prim_of[n][2] = square[:].rearrange("p c v -> p (c v)")
-            prim_of[n][5] = log_bf[:].rearrange("p c v -> p (c v)")
+        def times_coeffs(n):
+            for c, shares in enumerate(SHARES):
+                gate = gate_of[n][:, c].rearrange("p (j t k) -> p j t k", t=PACK, k=PRIMS)
+                coeff = coeff_of[n][:, c].rearrange("p t j k -> p j t k")
+                for engine, j_lo, j_hi in shares:
+                    multiplier = nc.gpsimd if engine == "gpsimd" else nc.vector
+                    multiplier.tensor_tensor(
+                        out=products(n, c, j_lo, j_hi),
+                        in0=gate[:, j_lo:j_hi, :, 1:PRIMS],
+                        in1=coeff[:, j_lo:j_hi, :, 1:PRIMS],
+                        op=ALU.mult,
+                    )
+
+        def log_on_gpsimd(n):
+            scratch = scratch_of[n + 1] if n + 1 < BATCHES else new_scratch(n + 1)
+            nc.gpsimd.tensor_scalar(
+                out=scratch[:, :X_COLS],
+                in0=ln_x_of[n][:],
+                scalar1=1.0,
+                scalar2=0.0,
+                op0=ALU.mult,
+                op1=ALU.add,
+            )
+            prim_of[n][5] = scratch[:, :X_COLS]
+            prim_of[n][2] = scratch[:, X_COLS:]
+
+        def square_x(n):
+            nc.vector.tensor_tensor(out=prim_of[n][2], in0=x_t_of[n], in1=x_t_of[n], op=ALU.mult)
 
         def primitives_exp_set(n):
             ln_x = ln_x_of[n]
@@ -215,10 +234,32 @@ def tile_dartslayer_k_kernel(tc, x, alphas, coeffs, out):
             )
             folded_of[n] = folded
 
+        def fold_x_on_vector(n):
+            folded = sbuf.tile([P, X_COLS], F32, bufs=2)
+            nc.vector.tensor_scalar(
+                out=folded[:],
+                in0=x_t_of[n],
+                scalar1=1.5 * math.pi,
+                scalar2=2.5 * math.pi,
+                op0=ALU.max,
+                op1=ALU.min,
+            )
+            nc.vector.scalar_tensor_tensor(
+                out=folded[:], in0=folded[:], scalar=2.0, in1=x_t_of[n], op0=ALU.mult, op1=ALU.subtract
+            )
+            folded_of[n] = folded
+
+        def on_vector(n):
+            return n % 3 == 2
+
         def primitive_sin(n):
             sine = sbuf.tile([P, X_COLS], BF16, bufs=2, align_bytes=64)
+            last_shift = 3 if on_vector(n) else 2
             nc.scalar.activation(
-                out=sine[:], in_=folded_of[n][:], func=ACT.Sin, bias=fold_shift[:, 2:3]
+                out=sine[:],
+                in_=folded_of[n][:],
+                func=ACT.Sin,
+                bias=fold_shift[:, last_shift : last_shift + 1],
             )
             prim_of[n][7] = sine[:]
 
@@ -258,17 +299,17 @@ def tile_dartslayer_k_kernel(tc, x, alphas, coeffs, out):
         def normalise(n):
             w = w_of[n]
             for c in range(PASSES):
-                product = gate_of[n][:, c, : GROUPS * CHANNELS].rearrange(
-                    "p (j t k) -> p j t k", t=PACK, k=CHANNELS
-                )
                 recip = recip_of[n][c][:].rearrange("p t j -> p j t").unsqueeze(3)
                 for k_lo, k_hi in ((0, 3), (3, 7)):
-                    nc.vector.tensor_tensor(
-                        out=w[:, k_lo:k_hi, c, :].rearrange("p k (j t) -> p j t k", t=PACK),
-                        in0=product[:, :, :, k_lo:k_hi],
-                        in1=recip.to_broadcast([P, J, PACK, k_hi - k_lo]),
-                        op=ALU.mult,
-                    )
+                    for engine, j_lo, j_hi in SHARES[c]:
+                        nc.vector.tensor_tensor(
+                            out=w[:, k_lo:k_hi, c, j_lo * PACK : j_hi * PACK].rearrange(
+                                "p k (j t) -> p j t k", t=PACK
+                            ),
+                            in0=products(n, c, j_lo, j_hi)[:, :, :, k_lo:k_hi],
+                            in1=recip[:, j_lo:j_hi].to_broadcast([P, j_hi - j_lo, PACK, k_hi - k_lo]),
+                            op=ALU.mult,
+                        )
             w_codes = sbuf.tile([P, CHANNELS, PASSES, J], U32, align_bytes=64)
             w_scales = sbuf.tile([P, CHANNELS, PASSES, J], U8, align_bytes=64)
             for ch in range(CHANNELS):
@@ -298,8 +339,6 @@ def tile_dartslayer_k_kernel(tc, x, alphas, coeffs, out):
                             stop=last,
                         )
 
-        folded_in = {0: (), 1: (1, 2)}
-
         def run(stage, n):
             if 0 <= n < BATCHES:
                 stage(n)
@@ -308,21 +347,21 @@ def tile_dartslayer_k_kernel(tc, x, alphas, coeffs, out):
             load_x(0)
             load_alphas(0)
             for n in range(-1, BATCHES + 1):
+                run(shift, n + 1)
                 run(reciprocal_total, n - 1)
                 run(normalise, n - 1)
-                run(primitives_on_gpsimd, n)
-                run(shift, n + 1)
+                run(log_on_gpsimd, n)
                 run(exponential, n)
                 run(load_alphas, n + 2)
                 run(transpose_x, n + 1)
                 run(load_x, n + 2)
                 run(total, n)
                 run(multiply, n - 1)
+                run(square_x, n)
                 run(times_coeffs, n)
                 run(load_coeffs, n + 1)
                 run(primitives_exp_set, n)
-                for m in folded_in.get(n, (n + 1,)):
-                    run(fold_x, m)
+                run(fold_x_on_vector if on_vector(n + 1) else fold_x, n + 1)
                 for m in (0,) if n == -1 else (n, n + 1) if n % 2 == 1 else ():
                     run(primitive_sin, m)
                 run(log_total, n)

@@ -23,7 +23,8 @@ BATCHES = I // I_BATCH
 HALVES = B // P
 X_COLS = PASSES * B * PACK
 GROUPS = J * PACK
-SHARES = ((("vector", 0, J),), (("vector", 0, 48), ("gpsimd", 48, J)))
+SHARES = ((("vector", 0, J),), (("vector", 0, J // 2), ("gpsimd", J // 2, J)))
+SINES_IN = {-1: (0,), 1: (1,), 2: (2, 3), 4: (4, 5), 6: (6, 7)}
 SAFE = 16.0
 
 FLOPS = 2 * B * J * I * CHANNELS
@@ -52,7 +53,7 @@ def tile_dartslayer_k_kernel(tc, x, alphas, coeffs, out):
 
         x_rows_of, x_t_of, ln_x_of, alpha_of, coeff_of = {}, {}, {}, {}, {}
         gate_of, total_of, prim_of, folded_of, p_mx_of, w_mx_of = {}, {}, {}, {}, {}, {}
-        recip_t_of, recip_of, w_of, scratch_of = {}, {}, {}, {}
+        recip_t_of, recip_of, scratch_of = {}, {}, {}
 
         def load_x(n):
             x_rows = sbuf.tile([P, HALVES, I_BATCH], BF16)
@@ -62,23 +63,27 @@ def tile_dartslayer_k_kernel(tc, x, alphas, coeffs, out):
             )
             x_rows_of[n] = x_rows
 
-        def load_weights(n, source, tiles, label, copies):
-            rows = sbuf.tile([P, PASSES, PACK, J, PRIMS], BF16, name=label, bufs=copies)
-            for c in range(PASSES):
-                first_row = (n * PASSES + c) * K_PASS
-                nc.sync.dma_start(
-                    out=rows[:, c].rearrange("p t j k -> p (t j k)"),
-                    in_=source[first_row : first_row + K_PASS].rearrange(
-                        "(p t) j k -> p (t j k)", p=P, t=PACK
-                    ),
-                )
-            tiles[n] = rows
+        def load_pass(rows, source, n, c):
+            first_row = (n * PASSES + c) * K_PASS
+            nc.sync.dma_start(
+                out=rows.rearrange("p t j k -> p (t j k)"),
+                in_=source[first_row : first_row + K_PASS].rearrange(
+                    "(p t) j k -> p (t j k)", p=P, t=PACK
+                ),
+            )
 
         def load_alphas(n):
-            load_weights(n, alphas, alpha_of, "alpha_rows", 2)
+            rows = sbuf.tile([P, PASSES, PACK, J, PRIMS], BF16, name="alpha_rows", bufs=2)
+            for c in range(PASSES):
+                load_pass(rows[:, c], alphas, n, c)
+            alpha_of[n] = rows
 
         def load_coeffs(n):
-            load_weights(n, coeffs, coeff_of, "coeff_rows", 1)
+            coeff_of[n] = []
+            for c in range(PASSES):
+                rows = sbuf.tile([P, PACK, J, PRIMS], BF16, name="coeff_rows%d" % c, bufs=1 + c)
+                load_pass(rows[:], coeffs, n, c)
+                coeff_of[n].append(rows[:])
 
         def transpose_x(n):
             words = x_rows_of[n][:].bitcast(F32)
@@ -183,24 +188,32 @@ def tile_dartslayer_k_kernel(tc, x, alphas, coeffs, out):
                 "p (j t k) -> p j t k", t=PACK, k=CHANNELS
             )
 
-        def times_coeffs(n):
+        def times_coeffs(n, who):
             for c, shares in enumerate(SHARES):
                 gate = gate_of[n][:, c].rearrange("p (j t k) -> p j t k", t=PACK, k=PRIMS)
-                coeff = coeff_of[n][:, c].rearrange("p t j k -> p j t k")
+                coeff = coeff_of[n][c].rearrange("p t j k -> p j t k")
                 for engine, j_lo, j_hi in shares:
-                    multiplier = nc.gpsimd if engine == "gpsimd" else nc.vector
-                    multiplier.tensor_tensor(
-                        out=products(n, c, j_lo, j_hi),
-                        in0=gate[:, j_lo:j_hi, :, 1:PRIMS],
-                        in1=coeff[:, j_lo:j_hi, :, 1:PRIMS],
-                        op=ALU.mult,
-                    )
+                    if engine == who:
+                        multiplier = nc.gpsimd if engine == "gpsimd" else nc.vector
+                        multiplier.tensor_tensor(
+                            out=products(n, c, j_lo, j_hi),
+                            in0=gate[:, j_lo:j_hi, :, 1:PRIMS],
+                            in1=coeff[:, j_lo:j_hi, :, 1:PRIMS],
+                            op=ALU.mult,
+                        )
 
-        def log_on_gpsimd(n):
-            scratch = scratch_of[n + 1] if n + 1 < BATCHES else new_scratch(n + 1)
+        def times_coeffs_on_vector(n):
+            times_coeffs(n, "vector")
+
+        def times_coeffs_on_gpsimd(n):
+            times_coeffs(n, "gpsimd")
+
+        def log_on_gpsimd(n, c):
+            scratch = scratch_of[n + 1] if n + 1 < BATCHES or c > 0 else new_scratch(n + 1)
+            half = slice(c * B * PACK, (c + 1) * B * PACK)
             nc.gpsimd.tensor_scalar(
-                out=scratch[:, :X_COLS],
-                in0=ln_x_of[n][:],
+                out=scratch[:, half],
+                in0=ln_x_of[n][:, half],
                 scalar1=1.0,
                 scalar2=0.0,
                 op0=ALU.mult,
@@ -208,6 +221,12 @@ def tile_dartslayer_k_kernel(tc, x, alphas, coeffs, out):
             )
             prim_of[n][5] = scratch[:, :X_COLS]
             prim_of[n][2] = scratch[:, X_COLS:]
+
+        def first_logs_on_gpsimd(n):
+            log_on_gpsimd(n, 0)
+
+        def last_logs_on_gpsimd(n):
+            log_on_gpsimd(n, 1)
 
         def square_x(n):
             nc.vector.tensor_tensor(out=prim_of[n][2], in0=x_t_of[n], in1=x_t_of[n], op=ALU.mult)
@@ -250,7 +269,7 @@ def tile_dartslayer_k_kernel(tc, x, alphas, coeffs, out):
             folded_of[n] = folded
 
         def on_vector(n):
-            return n % 3 == 2
+            return n % 4 == 2
 
         def primitive_sin(n):
             sine = sbuf.tile([P, X_COLS], BF16, bufs=2, align_bytes=64)
@@ -264,20 +283,18 @@ def tile_dartslayer_k_kernel(tc, x, alphas, coeffs, out):
             prim_of[n][7] = sine[:]
 
         def log_total(n):
-            w = sbuf.tile([P, CHANNELS, PASSES, GROUPS], BF16, align_bytes=64)
-            recip_t = w[:, CHANNELS - 2 :].rearrange("p k c g -> p (k c g)").bitcast(F32)
-            recip_t_of[n] = recip_t.rearrange("p (c g) -> p c g", c=PASSES)
-            w_of[n] = w
+            recip_t = sbuf.tile([P, PASSES, GROUPS], F32)
+            recip_t_of[n] = recip_t
             for c in range(PASSES):
                 nc.scalar.activation(
-                    out=recip_t_of[n][:, c],
+                    out=recip_t[:, c],
                     in_=total_of[n][c][:].rearrange("p t j -> p (t j)"),
                     func=ACT.Ln,
                 )
 
         def reciprocal_total(n):
             recip_t = recip_t_of[n]
-            nc.scalar.activation(out=recip_t, in_=recip_t, func=ACT.Exp, scale=-1.0)
+            nc.scalar.activation(out=recip_t[:], in_=recip_t[:], func=ACT.Exp, scale=-1.0)
             recip_of[n] = []
             for c in range(PASSES):
                 recip = psum.tile([P, PACK, P], F32, bufs=2)
@@ -297,19 +314,22 @@ def tile_dartslayer_k_kernel(tc, x, alphas, coeffs, out):
             p_mx_of[n] = (p_codes, p_scales)
 
         def normalise(n):
-            w = w_of[n]
-            for c in range(PASSES):
-                recip = recip_of[n][c][:].rearrange("p t j -> p j t").unsqueeze(3)
-                for k_lo, k_hi in ((0, 3), (3, 7)):
-                    for engine, j_lo, j_hi in SHARES[c]:
-                        nc.vector.tensor_tensor(
-                            out=w[:, k_lo:k_hi, c, j_lo * PACK : j_hi * PACK].rearrange(
-                                "p k (j t) -> p j t k", t=PACK
-                            ),
-                            in0=products(n, c, j_lo, j_hi)[:, :, :, k_lo:k_hi],
-                            in1=recip[:, j_lo:j_hi].to_broadcast([P, j_hi - j_lo, PACK, k_hi - k_lo]),
-                            op=ALU.mult,
-                        )
+            w = sbuf.tile([P, CHANNELS, PASSES, GROUPS], BF16, align_bytes=64)
+            for who in ("vector", "gpsimd"):
+                for c, shares in enumerate(SHARES):
+                    recip = recip_of[n][c][:].rearrange("p t j -> p j t").unsqueeze(3)
+                    for engine, j_lo, j_hi in shares:
+                        if engine != who:
+                            continue
+                        for k_lo, k_hi in ((0, 3), (3, 7)):
+                            nc.vector.tensor_tensor(
+                                out=w[:, k_lo:k_hi, c, j_lo * PACK : j_hi * PACK].rearrange(
+                                    "p k (j t) -> p j t k", t=PACK
+                                ),
+                                in0=products(n, c, j_lo, j_hi)[:, :, :, k_lo:k_hi],
+                                in1=recip[:, j_lo:j_hi].to_broadcast([P, j_hi - j_lo, PACK, k_hi - k_lo]),
+                                op=ALU.mult,
+                            )
             w_codes = sbuf.tile([P, CHANNELS, PASSES, J], U32, align_bytes=64)
             w_scales = sbuf.tile([P, CHANNELS, PASSES, J], U8, align_bytes=64)
             for ch in range(CHANNELS):
@@ -349,8 +369,10 @@ def tile_dartslayer_k_kernel(tc, x, alphas, coeffs, out):
             for n in range(-1, BATCHES + 1):
                 run(shift, n + 1)
                 run(reciprocal_total, n - 1)
+                run(first_logs_on_gpsimd, n)
+                run(times_coeffs_on_gpsimd, n - 1)
+                run(last_logs_on_gpsimd, n)
                 run(normalise, n - 1)
-                run(log_on_gpsimd, n)
                 run(exponential, n)
                 run(load_alphas, n + 2)
                 run(transpose_x, n + 1)
@@ -358,11 +380,11 @@ def tile_dartslayer_k_kernel(tc, x, alphas, coeffs, out):
                 run(total, n)
                 run(multiply, n - 1)
                 run(square_x, n)
-                run(times_coeffs, n)
+                run(times_coeffs_on_vector, n)
                 run(load_coeffs, n + 1)
                 run(primitives_exp_set, n)
                 run(fold_x_on_vector if on_vector(n + 1) else fold_x, n + 1)
-                for m in (0,) if n == -1 else (n, n + 1) if n % 2 == 1 else ():
+                for m in SINES_IN.get(n, ()):
                     run(primitive_sin, m)
                 run(log_total, n)
                 run(log_x, n + 1)

@@ -23,8 +23,10 @@ BATCHES = I // I_BATCH
 HALVES = B // P
 X_COLS = PASSES * B * PACK
 GROUPS = J * PACK
-SHARES = ((("vector", 0, J),), (("vector", 0, J // 2), ("gpsimd", J // 2, J)))
+SHARES = ((("vector", 0, J),), (("vector", 0, 48), ("gpsimd", 48, J)))
+FIRST_LOGS = 256
 SINES_IN = {-1: (0,), 1: (1,), 2: (2, 3), 4: (4, 5), 6: (6, 7)}
+SLOTS = (5, 1, 2, 3, 0, 4, 6)
 SAFE = 16.0
 
 FLOPS = 2 * B * J * I * CHANNELS
@@ -53,7 +55,7 @@ def tile_dartslayer_k_kernel(tc, x, alphas, coeffs, out):
 
         x_rows_of, x_t_of, ln_x_of, alpha_of, coeff_of = {}, {}, {}, {}, {}
         gate_of, total_of, prim_of, folded_of, p_mx_of, w_mx_of = {}, {}, {}, {}, {}, {}
-        recip_t_of, recip_of, scratch_of = {}, {}, {}
+        recip_t_of, recip_of, scratch_of, powers_of, w_of = {}, {}, {}, {}, {}
 
         def load_x(n):
             x_rows = sbuf.tile([P, HALVES, I_BATCH], BF16)
@@ -104,7 +106,7 @@ def tile_dartslayer_k_kernel(tc, x, alphas, coeffs, out):
                     in_=turned[:].rearrange("p h u b -> p h b u"),
                 )
             x_t_of[n] = x_t[:].rearrange("p c b t -> p (c b t)")
-            prim_of[n] = {1: x_t_of[n]}
+            prim_of[n] = {}
 
         def log_x(n):
             ln_x = sbuf.tile([P, X_COLS], F32)
@@ -208,40 +210,35 @@ def tile_dartslayer_k_kernel(tc, x, alphas, coeffs, out):
         def times_coeffs_on_gpsimd(n):
             times_coeffs(n, "gpsimd")
 
-        def log_on_gpsimd(n, c):
-            scratch = scratch_of[n + 1] if n + 1 < BATCHES or c > 0 else new_scratch(n + 1)
-            half = slice(c * B * PACK, (c + 1) * B * PACK)
+        def log_on_gpsimd(n, columns):
             nc.gpsimd.tensor_scalar(
-                out=scratch[:, half],
-                in0=ln_x_of[n][:, half],
+                out=prim_of[n][5][:, columns],
+                in0=ln_x_of[n][:, columns],
                 scalar1=1.0,
                 scalar2=0.0,
                 op0=ALU.mult,
                 op1=ALU.add,
             )
-            prim_of[n][5] = scratch[:, :X_COLS]
-            prim_of[n][2] = scratch[:, X_COLS:]
 
         def first_logs_on_gpsimd(n):
-            log_on_gpsimd(n, 0)
+            scratch = scratch_of[n + 1] if n + 1 < BATCHES else new_scratch(n + 1)
+            prim_of[n][5] = scratch[:, :X_COLS]
+            prim_of[n][2] = scratch[:, X_COLS:]
+            log_on_gpsimd(n, slice(0, FIRST_LOGS))
 
         def last_logs_on_gpsimd(n):
-            log_on_gpsimd(n, 1)
+            log_on_gpsimd(n, slice(FIRST_LOGS, X_COLS))
 
         def square_x(n):
             nc.vector.tensor_tensor(out=prim_of[n][2], in0=x_t_of[n], in1=x_t_of[n], op=ALU.mult)
 
         def primitives_exp_set(n):
-            ln_x = ln_x_of[n]
-            cube = sbuf.tile([P, X_COLS], BF16, align_bytes=64)
-            exp_x = sbuf.tile([P, X_COLS], BF16, align_bytes=64)
-            inverse = sbuf.tile([P, X_COLS], BF16, align_bytes=64)
-            nc.scalar.activation(out=inverse[:], in_=ln_x[:], func=ACT.Exp, scale=-1.0)
-            nc.scalar.activation(out=cube[:], in_=ln_x[:], func=ACT.Exp, scale=3.0)
-            nc.scalar.activation(out=exp_x[:], in_=x_t_of[n], func=ACT.Exp)
-            prim_of[n][3] = cube[:]
-            prim_of[n][4] = exp_x[:]
-            prim_of[n][6] = inverse[:]
+            powers = sbuf.tile([P, 3 * X_COLS], BF16, align_bytes=64)
+            cube, exp_x, inverse = (powers[:, q * X_COLS : (q + 1) * X_COLS] for q in range(3))
+            nc.scalar.activation(out=cube, in_=ln_x_of[n][:], func=ACT.Exp, scale=3.0)
+            nc.scalar.activation(out=exp_x, in_=x_t_of[n], func=ACT.Exp)
+            nc.scalar.activation(out=inverse, in_=ln_x_of[n][:], func=ACT.Exp, scale=-1.0)
+            powers_of[n] = powers
 
         def fold_x(n):
             folded = sbuf.tile([P, X_COLS], F32, bufs=2)
@@ -305,12 +302,21 @@ def tile_dartslayer_k_kernel(tc, x, alphas, coeffs, out):
         def quantise_x(n):
             p_codes = sbuf.tile([P, CHANNELS, PASSES, B], U32, align_bytes=64)
             p_scales = sbuf.tile([P, CHANNELS, PASSES, B], U8, align_bytes=64)
-            for ch in range(CHANNELS):
+            codes = p_codes[:].rearrange("p s c b -> p (s c b)")
+            scales = p_scales[:].rearrange("p s c b -> p (s c b)")
+            first = 0
+            for values in (
+                scratch_of[n + 1][:],
+                powers_of[n][:, : 2 * X_COLS],
+                powers_of[n][:, 2 * X_COLS :],
+                x_t_of[n],
+                prim_of[n][7],
+            ):
+                words = slice(first, first + values.shape[1] // PACK)
                 nc.vector.quantize_mx(
-                    out=p_codes[:, ch].rearrange("p c b -> p (c b)").bitcast(FP8X4),
-                    scales=p_scales[:, ch].rearrange("p c b -> p (c b)"),
-                    in_=prim_of[n][ch + 1],
+                    out=codes[:, words].bitcast(FP8X4), scales=scales[:, words], in_=values
                 )
+                first = words.stop
             p_mx_of[n] = (p_codes, p_scales)
 
         def normalise(n):
@@ -330,29 +336,34 @@ def tile_dartslayer_k_kernel(tc, x, alphas, coeffs, out):
                                 in1=recip[:, j_lo:j_hi].to_broadcast([P, j_hi - j_lo, PACK, k_hi - k_lo]),
                                 op=ALU.mult,
                             )
+            w_of[n] = w
+
+        def quantise_w(n):
+            w = w_of[n]
             w_codes = sbuf.tile([P, CHANNELS, PASSES, J], U32, align_bytes=64)
             w_scales = sbuf.tile([P, CHANNELS, PASSES, J], U8, align_bytes=64)
-            for ch in range(CHANNELS):
+            for lo in range(0, CHANNELS, 2):
+                some = slice(lo, min(lo + 2, CHANNELS))
                 nc.vector.quantize_mx(
-                    out=w_codes[:, ch].rearrange("p c j -> p (c j)").bitcast(FP8X4),
-                    scales=w_scales[:, ch].rearrange("p c j -> p (c j)"),
-                    in_=w[:, ch].rearrange("p c g -> p (c g)"),
+                    out=w_codes[:, some].rearrange("p k c j -> p (k c j)").bitcast(FP8X4),
+                    scales=w_scales[:, some].rearrange("p k c j -> p (k c j)"),
+                    in_=w[:, some].rearrange("p k c g -> p (k c g)"),
                 )
             w_mx_of[n] = (w_codes, w_scales)
 
         def multiply(n):
             p_codes, p_scales = p_mx_of[n]
             w_codes, w_scales = w_mx_of[n]
-            for c in range(PASSES):
-                for ch in range(CHANNELS):
+            for ch in range(CHANNELS):
+                for c in range(PASSES):
                     first = n == 0 and c == 0 and ch == 0
                     last = n == BATCHES - 1 and c == PASSES - 1 and ch == CHANNELS - 1
                     for h in range(HALVES):
                         rows = slice(h * P, (h + 1) * P)
                         nc.tensor.matmul_mx(
                             out=acc[h][:],
-                            lhsT=p_codes[:, ch, c, rows].bitcast(FP8X4),
-                            lhsT_scale=p_scales[:, ch, c, rows],
+                            lhsT=p_codes[:, SLOTS[ch], c, rows].bitcast(FP8X4),
+                            lhsT_scale=p_scales[:, SLOTS[ch], c, rows],
                             rhs=w_codes[:, ch, c, :].bitcast(FP8X4),
                             rhs_scale=w_scales[:, ch, c, :],
                             start=first,
@@ -372,23 +383,30 @@ def tile_dartslayer_k_kernel(tc, x, alphas, coeffs, out):
                 run(first_logs_on_gpsimd, n)
                 run(times_coeffs_on_gpsimd, n - 1)
                 run(last_logs_on_gpsimd, n)
+                if n == BATCHES:
+                    run(primitives_exp_set, n - 1)
                 run(normalise, n - 1)
+                if n == BATCHES:
+                    run(quantise_x, n - 1)
+                run(square_x, n)
+                run(quantise_w, n - 1)
                 run(exponential, n)
                 run(load_alphas, n + 2)
                 run(transpose_x, n + 1)
                 run(load_x, n + 2)
                 run(total, n)
                 run(multiply, n - 1)
-                run(square_x, n)
                 run(times_coeffs_on_vector, n)
                 run(load_coeffs, n + 1)
-                run(primitives_exp_set, n)
+                if n < BATCHES - 1:
+                    run(primitives_exp_set, n)
                 run(fold_x_on_vector if on_vector(n + 1) else fold_x, n + 1)
                 for m in SINES_IN.get(n, ()):
                     run(primitive_sin, m)
                 run(log_total, n)
                 run(log_x, n + 1)
-                run(quantise_x, n)
+                if n < BATCHES - 1:
+                    run(quantise_x, n)
             for h in range(HALVES):
                 result = sbuf.tile([P, J], F32, bufs=2)
                 nc.vector.tensor_copy(out=result[:], in_=acc[h][:])

import math
from contextlib import ExitStack

import concourse.mybir as mybir
from concourse.masks import make_identity

BF16 = mybir.dt.bfloat16
F32 = mybir.dt.float32
U32 = mybir.dt.uint32
U8 = mybir.dt.uint8
FP8X4 = mybir.dt.float8_e4m3fn_x4
ACT = mybir.ActivationFunctionType
ALU = mybir.AluOpType

B, I, J, PRIMS = 256, 8192, 128, 8
CHANNELS = PRIMS - 1
P = 128
PACK = 4
K_PASS = P * PACK
PASSES = 2
I_BATCH = PASSES * K_PASS
BATCHES = I // I_BATCH
HALVES = B // P
X_COLS = PASSES * B * PACK
GROUPS = J * PACK
SHARES = ((("vector", 0, J),), (("vector", 0, 48), ("gpsimd", 48, J)))
FIRST_LOGS = 256
SINES_IN = {-1: (0,), 1: (1,), 2: (2, 3), 4: (4, 5), 6: (6, 7)}
SLOTS = (5, 1, 2, 3, 0, 4, 6)
SAFE = 16.0

FLOPS = 2 * B * J * I * CHANNELS


def tile_dartslayer_k_kernel(tc, x, alphas, coeffs, out):
    nc = tc.nc
    with ExitStack() as ctx:
        sbuf = ctx.enter_context(tc.tile_pool(name="sbuf", bufs=1))
        psum = ctx.enter_context(tc.psum_pool(name="psum", bufs=1))

        identity = sbuf.tile([P, P], F32)
        make_identity(nc, identity[:])
        zero = sbuf.tile([P, 1], F32)
        nc.vector.memset(zero[:], 0.0)
        fold_shift = sbuf.tile([P, 4], F32)
        for place, turns in enumerate((2.5, 1.0, 0.5, 2.0)):
            nc.vector.tensor_scalar_add(
                out=fold_shift[:, place : place + 1], in0=zero[:], scalar1=-turns * math.pi
            )

        acc = []
        for h in range(HALVES):
            acc_h = psum.tile([P, J], F32, name="acc%d" % h)
            acc.append(acc_h)

        x_rows_of, x_t_of, ln_x_of, alpha_of, coeff_of = {}, {}, {}, {}, {}
        gate_of, total_of, prim_of, folded_of, p_mx_of, w_mx_of = {}, {}, {}, {}, {}, {}
        recip_t_of, recip_of, scratch_of, powers_of, w_of = {}, {}, {}, {}, {}

        def load_x(n):
            x_rows = sbuf.tile([P, HALVES, I_BATCH], BF16)
            nc.sync.dma_start(
                out=x_rows[:],
                in_=x[:, n * I_BATCH : (n + 1) * I_BATCH].rearrange("(h b) i -> b h i", h=HALVES),
            )
            x_rows_of[n] = x_rows

        def load_pass(rows, source, n, c):
            first_row = (n * PASSES + c) * K_PASS
            nc.sync.dma_start(
                out=rows.rearrange("p t j k -> p (t j k)"),
                in_=source[first_row : first_row + K_PASS].rearrange(
                    "(p t) j k -> p (t j k)", p=P, t=PACK
                ),
            )

        def load_alphas(n):
            rows = sbuf.tile([P, PASSES, PACK, J, PRIMS], BF16, name="alpha_rows", bufs=2)
            for c in range(PASSES):
                load_pass(rows[:, c], alphas, n, c)
            alpha_of[n] = rows

        def load_coeffs(n):
            coeff_of[n] = []
            for c in range(PASSES):
                rows = sbuf.tile([P, PACK, J, PRIMS], BF16, name="coeff_rows%d" % c, bufs=1 + c)
                load_pass(rows[:], coeffs, n, c)
                coeff_of[n].append(rows[:])

        def transpose_x(n):
            words = x_rows_of[n][:].bitcast(F32)
            x_t = sbuf.tile([P, PASSES, B, PACK], BF16, bufs=2, align_bytes=64)
            x_t_words = x_t[:].bitcast(F32)
            pass_words = K_PASS // 2
            for c in range(PASSES):
                turned = psum.tile([P, HALVES, 2, P], F32, bufs=2)
                for h in range(HALVES):
                    for u in range(2):
                        nc.tensor.transpose(
                            turned[:, h, u, :],
                            words[:, h, c * pass_words + u : (c + 1) * pass_words : 2],
                            identity[:],
                        )
                nc.scalar.copy(
                    out=x_t_words[:, c].rearrange("p (h b) u -> p h b u", h=HALVES),
                    in_=turned[:].rearrange("p h u b -> p h b u"),
                )
            x_t_of[n] = x_t[:].rearrange("p c b t -> p (c b t)")
            prim_of[n] = {}

        def log_x(n):
            ln_x = sbuf.tile([P, X_COLS], F32)
            nc.scalar.activation(out=ln_x[:], in_=x_t_of[n], func=ACT.Ln)
            ln_x_of[n] = ln_x

        def new_scratch(n):
            scratch = sbuf.tile([P, PASSES * GROUPS * 4], BF16, align_bytes=64)
            scratch_of[n] = scratch
            return scratch

        def shift(n):
            rows = alpha_of[n]
            scratch = new_scratch(n)
            max4 = scratch[:].rearrange("p (c g k) -> p c g k", c=PASSES, k=4)
            max2 = sbuf.tile([P, PASSES, GROUPS, 2], BF16)
            max1 = [
                max4[:, c].rearrange("p g k -> p (g k)")[:, : GROUPS * 2].rearrange("p (g u) -> p g u", u=2)
                for c in range(PASSES)
            ]
            by_group = [rows[:, c].rearrange("p t j k -> p (t j) k") for c in range(PASSES)]
            for c in range(PASSES):
                nc.vector.tensor_tensor(
                    out=max4[:, c], in0=by_group[c][:, :, 0:4], in1=by_group[c][:, :, 4:8], op=ALU.max
                )
            for c in range(PASSES):
                nc.vector.tensor_tensor(
                    out=max2[:, c], in0=max4[:, c, :, 0:2], in1=max4[:, c, :, 2:4], op=ALU.max
                )
            for c in range(PASSES):
                nc.vector.tensor_tensor(
                    out=max1[c], in0=max2[:, c], in1=max2[:, c, :, ::-1], op=ALU.max
                )
            for c in range(PASSES):
                nc.vector.tensor_scalar(
                    out=max2[:, c], in0=max1[c], scalar1=-SAFE, scalar2=SAFE, op0=ALU.max, op1=ALU.min
                )
            for c in range(PASSES):
                nc.vector.tensor_tensor(
                    out=max1[c], in0=max1[c], in1=max2[:, c], op=ALU.subtract
                )
            for c in range(PASSES):
                nc.vector.tensor_tensor(
                    out=by_group[c].rearrange("p g (h u) -> p g h u", u=2),
                    in0=by_group[c].rearrange("p g (h u) -> p g h u", u=2),
                    in1=max1[c].unsqueeze(2).to_broadcast([P, GROUPS, PRIMS // 2, 2]),
                    op=ALU.subtract,
                )

        def exponential(n):
            gate = sbuf.tile([P, PASSES, GROUPS * PRIMS], F32, bufs=2)
            for c in range(PASSES):
                nc.scalar.activation(
                    out=gate[:, c].rearrange("p (j t k) -> p j t k", t=PACK, k=PRIMS),
                    in_=alpha_of[n][:, c].rearrange("p t j k -> p j t k"),
                    func=ACT.Exp,
                )
            gate_of[n] = gate

        def total(n):
            total_of[n] = []
            for c in range(PASSES):
                gate = gate_of[n][:, c].rearrange("p (j t k) -> p j t k", t=PACK, k=PRIMS)
                sums_t = psum.tile([P, PACK, P], F32, bufs=2)
                for t in range(PACK):
                    for k in range(PRIMS):
                        nc.tensor.matmul(
                            out=sums_t[:, t, :],
                            lhsT=gate[:, :, t, k],
                            rhs=identity[:],
                            is_transpose=True,
                            start=(k == 0),
                            stop=(k == PRIMS - 1),
                        )
                total_of[n].append(sums_t)

        def products(n, c, j_lo, j_hi):
            first = j_lo * PACK * PRIMS
            size = (j_hi - j_lo) * PACK * CHANNELS
            return gate_of[n][:, c, first : first + size].rearrange(
                "p (j t k) -> p j t k", t=PACK, k=CHANNELS
            )

        def times_coeffs(n, who):
            for c, shares in enumerate(SHARES):
                gate = gate_of[n][:, c].rearrange("p (j t k) -> p j t k", t=PACK, k=PRIMS)
                coeff = coeff_of[n][c].rearrange("p t j k -> p j t k")
                for engine, j_lo, j_hi in shares:
                    if engine == who:
                        multiplier = nc.gpsimd if engine == "gpsimd" else nc.vector
                        multiplier.tensor_tensor(
                            out=products(n, c, j_lo, j_hi),
                            in0=gate[:, j_lo:j_hi, :, 1:PRIMS],
                            in1=coeff[:, j_lo:j_hi, :, 1:PRIMS],
                            op=ALU.mult,
                        )

        def times_coeffs_on_vector(n):
            times_coeffs(n, "vector")

        def times_coeffs_on_gpsimd(n):
            times_coeffs(n, "gpsimd")

        def log_on_gpsimd(n, columns):
            nc.gpsimd.tensor_scalar(
                out=prim_of[n][5][:, columns],
                in0=ln_x_of[n][:, columns],
                scalar1=1.0,
                scalar2=0.0,
                op0=ALU.mult,
                op1=ALU.add,
            )

        def first_logs_on_gpsimd(n):
            scratch = scratch_of[n + 1] if n + 1 < BATCHES else new_scratch(n + 1)
            prim_of[n][5] = scratch[:, :X_COLS]
            prim_of[n][2] = scratch[:, X_COLS:]
            log_on_gpsimd(n, slice(0, FIRST_LOGS))

        def last_logs_on_gpsimd(n):
            log_on_gpsimd(n, slice(FIRST_LOGS, X_COLS))

        def square_x(n):
            nc.vector.tensor_tensor(out=prim_of[n][2], in0=x_t_of[n], in1=x_t_of[n], op=ALU.mult)

        def primitives_exp_set(n):
            powers = sbuf.tile([P, 3 * X_COLS], BF16, align_bytes=64)
            cube, exp_x, inverse = (powers[:, q * X_COLS : (q + 1) * X_COLS] for q in range(3))
            nc.scalar.activation(out=cube, in_=ln_x_of[n][:], func=ACT.Exp, scale=3.0)
            nc.scalar.activation(out=exp_x, in_=x_t_of[n], func=ACT.Exp)
            nc.scalar.activation(out=inverse, in_=ln_x_of[n][:], func=ACT.Exp, scale=-1.0)
            powers_of[n] = powers

        def fold_x(n):
            folded = sbuf.tile([P, X_COLS], F32, bufs=2)
            nc.scalar.activation(
                out=folded[:], in_=x_t_of[n], func=ACT.Abs, bias=fold_shift[:, 0:1]
            )
            nc.scalar.activation(
                out=folded[:], in_=folded[:], func=ACT.Abs, bias=fold_shift[:, 1:2]
            )
            folded_of[n] = folded

        def fold_x_on_vector(n):
            folded = sbuf.tile([P, X_COLS], F32, bufs=2)
            nc.vector.tensor_scalar(
                out=folded[:],
                in0=x_t_of[n],
                scalar1=1.5 * math.pi,
                scalar2=2.5 * math.pi,
                op0=ALU.max,
                op1=ALU.min,
            )
            nc.vector.scalar_tensor_tensor(
                out=folded[:], in0=folded[:], scalar=2.0, in1=x_t_of[n], op0=ALU.mult, op1=ALU.subtract
            )
            folded_of[n] = folded

        def on_vector(n):
            return n % 4 == 2

        def primitive_sin(n):
            sine = sbuf.tile([P, X_COLS], BF16, bufs=2, align_bytes=64)
            last_shift = 3 if on_vector(n) else 2
            nc.scalar.activation(
                out=sine[:],
                in_=folded_of[n][:],
                func=ACT.Sin,
                bias=fold_shift[:, last_shift : last_shift + 1],
            )
            prim_of[n][7] = sine[:]

        def log_total(n):
            recip_t = sbuf.tile([P, PASSES, GROUPS], F32)
            recip_t_of[n] = recip_t
            for c in range(PASSES):
                nc.scalar.activation(
                    out=recip_t[:, c],
                    in_=total_of[n][c][:].rearrange("p t j -> p (t j)"),
                    func=ACT.Ln,
                )

        def reciprocal_total(n):
            recip_t = recip_t_of[n]
            nc.scalar.activation(out=recip_t[:], in_=recip_t[:], func=ACT.Exp, scale=-1.0)
            recip_of[n] = []
            for c in range(PASSES):
                recip = psum.tile([P, PACK, P], F32, bufs=2)
                for t in range(PACK):
                    nc.tensor.transpose(recip[:, t, :], recip_t[:, c, t * P : (t + 1) * P], identity[:])
                recip_of[n].append(recip)

        def quantise_x(n):
            p_codes = sbuf.tile([P, CHANNELS, PASSES, B], U32, align_bytes=64)
            p_scales = sbuf.tile([P, CHANNELS, PASSES, B], U8, align_bytes=64)
            codes = p_codes[:].rearrange("p s c b -> p (s c b)")
            scales = p_scales[:].rearrange("p s c b -> p (s c b)")
            first = 0
            for values in (
                scratch_of[n + 1][:],
                powers_of[n][:, : 2 * X_COLS],
                powers_of[n][:, 2 * X_COLS :],
                x_t_of[n],
                prim_of[n][7],
            ):
                words = slice(first, first + values.shape[1] // PACK)
                nc.vector.quantize_mx(
                    out=codes[:, words].bitcast(FP8X4), scales=scales[:, words], in_=values
                )
                first = words.stop
            p_mx_of[n] = (p_codes, p_scales)

        def normalise(n):
            w = sbuf.tile([P, CHANNELS, PASSES, GROUPS], BF16, align_bytes=64)
            for who in ("vector", "gpsimd"):
                for c, shares in enumerate(SHARES):
                    recip = recip_of[n][c][:].rearrange("p t j -> p j t").unsqueeze(3)
                    for engine, j_lo, j_hi in shares:
                        if engine != who:
                            continue
                        for k_lo, k_hi in ((0, 3), (3, 7)):
                            nc.vector.tensor_tensor(
                                out=w[:, k_lo:k_hi, c, j_lo * PACK : j_hi * PACK].rearrange(
                                    "p k (j t) -> p j t k", t=PACK
                                ),
                                in0=products(n, c, j_lo, j_hi)[:, :, :, k_lo:k_hi],
                                in1=recip[:, j_lo:j_hi].to_broadcast([P, j_hi - j_lo, PACK, k_hi - k_lo]),
                                op=ALU.mult,
                            )
            w_of[n] = w

        def quantise_w(n):
            w = w_of[n]
            w_codes = sbuf.tile([P, CHANNELS, PASSES, J], U32, align_bytes=64)
            w_scales = sbuf.tile([P, CHANNELS, PASSES, J], U8, align_bytes=64)
            for lo in range(0, CHANNELS, 2):
                some = slice(lo, min(lo + 2, CHANNELS))
                nc.vector.quantize_mx(
                    out=w_codes[:, some].rearrange("p k c j -> p (k c j)").bitcast(FP8X4),
                    scales=w_scales[:, some].rearrange("p k c j -> p (k c j)"),
                    in_=w[:, some].rearrange("p k c g -> p (k c g)"),
                )
            w_mx_of[n] = (w_codes, w_scales)

        def multiply(n):
            p_codes, p_scales = p_mx_of[n]
            w_codes, w_scales = w_mx_of[n]
            for ch in range(CHANNELS):
                for c in range(PASSES):
                    first = n == 0 and c == 0 and ch == 0
                    last = n == BATCHES - 1 and c == PASSES - 1 and ch == CHANNELS - 1
                    for h in range(HALVES):
                        rows = slice(h * P, (h + 1) * P)
                        nc.tensor.matmul_mx(
                            out=acc[h][:],
                            lhsT=p_codes[:, SLOTS[ch], c, rows].bitcast(FP8X4),
                            lhsT_scale=p_scales[:, SLOTS[ch], c, rows],
                            rhs=w_codes[:, ch, c, :].bitcast(FP8X4),
                            rhs_scale=w_scales[:, ch, c, :],
                            start=first,
                            stop=last,
                        )

        def run(stage, n):
            if 0 <= n < BATCHES:
                stage(n)

        with tc.manual_schedule():
            load_x(0)
            load_alphas(0)
            for n in range(-1, BATCHES + 1):
                run(shift, n + 1)
                run(reciprocal_total, n - 1)
                run(first_logs_on_gpsimd, n)
                run(times_coeffs_on_gpsimd, n - 1)
                run(last_logs_on_gpsimd, n)
                if n == BATCHES:
                    run(primitives_exp_set, n - 1)
                run(normalise, n - 1)
                if n == BATCHES:
                    run(quantise_x, n - 1)
                run(square_x, n)
                run(quantise_w, n - 1)
                run(exponential, n)
                run(load_alphas, n + 2)
                run(transpose_x, n + 1)
                run(load_x, n + 2)
                run(total, n)
                run(multiply, n - 1)
                run(times_coeffs_on_vector, n)
                run(load_coeffs, n + 1)
                if n < BATCHES - 1:
                    run(primitives_exp_set, n)
                run(fold_x_on_vector if on_vector(n + 1) else fold_x, n + 1)
                for m in SINES_IN.get(n, ()):
                    run(primitive_sin, m)
                run(log_total, n)
                run(log_x, n + 1)
                if n < BATCHES - 1:
                    run(quantise_x, n)
            for h in range(HALVES):
                result = sbuf.tile([P, J], F32, bufs=2)
                nc.vector.tensor_copy(out=result[:], in_=acc[h][:])
                nc.sync.dma_start(out=out[h * P : (h + 1) * P, :], in_=result[:])
